import numpy as np
import ml_dtypes


def mxq(x, axis, fmt="e4m3"):
    dtype, down = {"e4m3": (ml_dtypes.float8_e4m3fn, 7), "e5m2": (ml_dtypes.float8_e5m2, 14)}[fmt]
    v = np.moveaxis(np.asarray(x, np.float32).astype(ml_dtypes.bfloat16).astype(np.float64), axis, -1)
    blocks = v.reshape(v.shape[:-1] + (-1, 32))
    amax = np.abs(blocks).max(-1, keepdims=True)
    byte = np.maximum(np.where(amax > 0, np.frexp(amax)[1] - 1 + 127, 0) - down, 1)
    scale = np.exp2(byte - 127.0)
    codes = (blocks / scale).astype(np.float32).astype(dtype).astype(np.float64)
    return np.moveaxis((codes * scale).reshape(v.shape), -1, axis)


WIDE = False


def mx_kscale(k):
    if not WIDE:
        return np.ones(k)
    levels = np.array([10, -10, 5, -5, 0])
    a = np.random.permutation(np.resize(levels, k // 512 * 4)).reshape(k // 512, 4)
    idx = np.arange(k)
    return np.exp2(a[idx // 512, idx % 128 // 32])


BF16 = ml_dtypes.bfloat16


def bf(x):
    return np.asarray(x, np.float32).astype(BF16)


def f64(x):
    return np.asarray(x).astype(np.float64)


E2M1 = np.array([0.0, 0.5, 1.0, 1.5, 2.0, 3.0, 4.0, 6.0, -0.0, -0.5, -1.0, -1.5, -2.0, -3.0, -4.0, -6.0])


def pack_weight(w, fmt):
    k, n = w.shape
    w = f64(bf(w)).reshape(k // 32, 32, n)
    amax = np.abs(w).max(1)
    if fmt == "e4m3":
        byte = np.frexp(amax)[1] - 1 + 127 - 7
    else:
        mant, ex = np.frexp(amax / 6.0)
        byte = np.where(mant > 0.5, ex, ex - 1) + 127
    byte = np.clip(np.where(amax > 0, byte, 1), 1, 254)
    scaled = (w * np.exp2(127.0 - byte)[:, None, :]).reshape(k, n).astype(np.float32)
    by_word = np.ascontiguousarray(scaled.reshape(k // 512, 128, 4, n).transpose(0, 1, 3, 2))
    if fmt == "e4m3":
        words = by_word.astype(ml_dtypes.float8_e4m3fn).view(np.uint8)
    else:
        c = by_word.astype(ml_dtypes.float4_e2m1fn).view(np.uint8) & 0xF
        words = c[..., 0::2] | (c[..., 1::2] << 4)
    return np.ascontiguousarray(words), np.ascontiguousarray(byte.astype(np.uint8).reshape(k // 512, 16, n))


def unpack_weight(words, scales, fmt):
    g, p, n, _ = words.shape
    if fmt == "e4m3":
        vals = np.ascontiguousarray(words).view(ml_dtypes.float8_e4m3fn).astype(np.float64)
    else:
        nib = np.empty((g, p, n, 4), np.uint8)
        nib[..., 0::2] = words & 0xF
        nib[..., 1::2] = words >> 4
        vals = E2M1[nib]
    vals = vals * np.repeat(np.exp2(scales.astype(np.float64) - 127.0), 8, axis=1)[..., None]
    return vals.transpose(0, 1, 3, 2).reshape(g * 512, n)

def pack4(w):
    words, scales = pack_weight(w, "e2m1")
    return words.reshape(words.shape[0], 128, -1), scales


def unpack4(words, scales):
    return unpack_weight(words.reshape(words.shape[0], 128, -1, 2), scales, "e2m1")


B, K, N = 2048, 512, 1024
NACT = 4


def setup_inputs():
    s = mx_kscale(K)
    g = np.tile(np.array([1.0, 1.0, 1.0, 0.5]), N // NACT)
    x = np.random.standard_normal((B, K)) * s
    weight = np.random.uniform(-1.0, 1.0, (N, K)) / np.sqrt(K) * g[:, None] / s[None, :]
    words, scales = pack4(weight.T)
    return {"x": bf(x), "weight_words": words, "weight_scales": scales}


def reference(x, weight_words, weight_scales):
    y = mxq(f64(x), 1, "e4m3") @ unpack4(weight_words, weight_scales)
    rows, cols = y.shape
    y3 = y.reshape(rows, cols // NACT, NACT)
    out = np.stack(
        [y3[..., 0],
         np.cos(y3[..., 1]),
         np.sin(y3[..., 2]),
         np.tan(y3[..., 3])],
        axis=-1,
    )
    return out.reshape(rows, cols)

@@ -1,0 +1,132 @@
+from contextlib import ExitStack
+
+import concourse.mybir as mybir
+from concourse.masks import make_identity
+
+F32 = mybir.dt.float32
+BF16 = mybir.dt.bfloat16
+I32 = mybir.dt.int32
+U32 = mybir.dt.uint32
+U8 = mybir.dt.uint8
+FP8X4 = mybir.dt.float8_e4m3fn_x4
+FP4X4 = mybir.dt.float4_e2m1fn_x4
+ACT = mybir.ActivationFunctionType
+ALU = mybir.AluOpType
+
+P = 128
+B, K, N = 2048, 512, 1024
+BLOCKS = B // P
+BANK = 512
+HALVES = N // BANK
+KINDS = 4
+PER_BANK = BANK // KINDS
+PER_BLOCK = N // KINDS
+WORDS = K // 2
+LOAD_BLOCKS = 4
+
+LIN, COS, SIN, TAN, COS_T, SIN_T = 0, 1, 2, 3, 4, 5
+
+FLOPS = 2 * B * K * N
+
+
+def tile_mylayerfunc_kernel(tc, x, weight_words, weight_scales, out):
+    nc = tc.nc
+    x_blocks = x.rearrange("(p m) k -> p m k", m=BLOCKS)
+    out_blocks = out.rearrange("(p m) n -> p m n", m=BLOCKS)
+
+    with ExitStack() as ctx:
+        keep = ctx.enter_context(tc.tile_pool(name="keep", bufs=1))
+        stage = ctx.enter_context(tc.tile_pool(name="stage", bufs=2))
+        work = ctx.enter_context(tc.tile_pool(name="work", bufs=3))
+        psum_x = ctx.enter_context(tc.psum_pool(name="psum_x", bufs=2))
+        psum_y = ctx.enter_context(tc.psum_pool(name="psum_y", bufs=6))
+
+        table_warm = keep.tile([P, 1], F32)
+        nc.vector.memset(table_warm[:], 0.0)
+        nc.scalar.activation(out=table_warm[:], in_=table_warm[:], func=ACT.Sin)
+
+        w_scales = keep.tile([P, N], U8, align_bytes=64)
+        nc.vector.memset(w_scales[:].bitcast(I32), 0)
+        ident = keep.tile([P, P], F32)
+        make_identity(nc, ident[:])
+
+        x_sb = keep.tile([P, BLOCKS, K], BF16)
+        w_words = keep.tile([P, 2 * N], U8, align_bytes=64)
+
+        def load_x(first):
+            blocks = slice(first, first + LOAD_BLOCKS)
+            nc.sync.dma_start(out=x_sb[:, blocks, :], in_=x_blocks[:, blocks, :])
+
+        load_x(0)
+        for quad in range(4):
+            nc.sync.dma_start(
+                out=w_scales[32 * quad : 32 * quad + 4, :].bitcast(I32),
+                in_=weight_scales[0, 4 * quad : 4 * quad + 4, :].bitcast(I32),
+            )
+        nc.sync.dma_start(out=w_words[:].bitcast(I32), in_=weight_words[0].bitcast(I32))
+        for first in range(LOAD_BLOCKS, BLOCKS, LOAD_BLOCKS):
+            load_x(first)
+
+        x_codes = keep.tile([P, BLOCKS * P], U32, align_bytes=64)
+        x_scales = keep.tile([P, BLOCKS * P], U8, align_bytes=64)
+
+        def quantise_two_blocks(first):
+            xt = psum_x.tile([P, 2, 2, P], F32)
+            for i in range(2):
+                words = x_sb[:, first + i, :].bitcast(F32)
+                for u in range(2):
+                    nc.tensor.transpose(out=xt[:, i, u, :], in_=words[:, u:WORDS:2], identity=ident[:])
+            grouped = stage.tile([P, 2 * P * 4], BF16, align_bytes=64)
+            nc.vector.tensor_copy(
+                out=grouped[:].bitcast(F32).rearrange("p (i r u) -> p i r u", i=2, u=2),
+                in_=xt[:].rearrange("p i u r -> p i r u"),
+            )
+            cols = slice(first * P, (first + 2) * P)
+            nc.vector.quantize_mx(
+                out=x_codes[:, cols].bitcast(FP8X4), scales=x_scales[:, cols], in_=grouped[:]
+            )
+
+        def one_block(m):
+            planes = work.tile([P, 6, PER_BLOCK], F32)
+            half_sin = work.tile([P, 2, PER_BLOCK], F32)
+            rows = slice(m * P, (m + 1) * P)
+            for h in range(HALVES):
+                y = psum_y.tile([P, BANK], F32)
+                nc.tensor.matmul_mx(
+                    out=y[:],
+                    lhsT=x_codes[:, rows].bitcast(FP8X4),
+                    lhsT_scale=x_scales[:, rows],
+                    rhs=w_words[:, 2 * BANK * h : 2 * BANK * (h + 1)].bitcast(FP4X4),
+                    rhs_scale=w_scales[:, BANK * h : BANK * (h + 1)],
+                    start=True,
+                    stop=True,
+                )
+                by_kind = y[:].rearrange("p (j c) -> p c j", c=KINDS)
+                js = slice(h * PER_BANK, (h + 1) * PER_BANK)
+                nc.scalar.activation(out=half_sin[:, :, js], in_=by_kind[:, COS : TAN + 1 : 2, :], func=ACT.Sin, scale=0.5)
+                nc.scalar.activation(out=planes[:, SIN : SIN_T + 1 : 3, js], in_=by_kind[:, SIN : TAN + 1, :], func=ACT.Sin)
+                nc.scalar.copy(out=planes[:, LIN, js], in_=by_kind[:, LIN, :])
+            nc.scalar.activation(out=half_sin[:], in_=half_sin[:], func=ACT.Square)
+            nc.vector.tensor_scalar(
+                out=planes[:, COS : COS_T + 1 : 3, :], in0=half_sin[:], scalar1=-2.0, scalar2=1.0, op0=ALU.mult, op1=ALU.add
+            )
+            inv_cos = work.tile([P, PER_BLOCK], F32)
+            nc.vector.reciprocal(out=inv_cos[:], in_=planes[:, COS_T, :])
+            nc.gpsimd.tensor_tensor(out=planes[:, TAN, :], in0=planes[:, SIN_T, :], in1=inv_cos[:], op=ALU.mult)
+            woven = work.tile([P, N], F32)
+            nc.gpsimd.tensor_scalar(
+                out=woven[:].rearrange("p (j c) -> p j c", c=KINDS),
+                in0=planes[:, LIN : TAN + 1, :].rearrange("p c j -> p j c"),
+                scalar1=1.0,
+                scalar2=0.0,
+                op0=ALU.mult,
+                op1=ALU.add,
+            )
+            nc.sync.dma_start(out=out_blocks[:, m, :], in_=woven[:])
+
+        quantise_two_blocks(0)
+        for first in range(0, BLOCKS, 2):
+            if first + 2 < BLOCKS:
+                quantise_two_blocks(first + 2)
+            one_block(first)
+            one_block(first + 1)

@@ -1,3 +1,4 @@
+import math
 from contextlib import ExitStack
 
 import concourse.mybir as mybir
@@ -37,7 +38,7 @@ def tile_mylayerfunc_kernel(tc, x, weight_words, weight_scales, out):
     with ExitStack() as ctx:
         keep = ctx.enter_context(tc.tile_pool(name="keep", bufs=1))
         stage = ctx.enter_context(tc.tile_pool(name="stage", bufs=2))
-        work = ctx.enter_context(tc.tile_pool(name="work", bufs=3))
+        work = ctx.enter_context(tc.tile_pool(name="work", bufs=6))
         psum_x = ctx.enter_context(tc.psum_pool(name="psum_x", bufs=2))
         psum_y = ctx.enter_context(tc.psum_pool(name="psum_y", bufs=6))
 
@@ -53,19 +54,20 @@ def tile_mylayerfunc_kernel(tc, x, weight_words, weight_scales, out):
         x_sb = keep.tile([P, BLOCKS, K], BF16)
         w_words = keep.tile([P, 2 * N], U8, align_bytes=64)
 
-        def load_x(first):
-            blocks = slice(first, first + LOAD_BLOCKS)
+        def load_x(first, count):
+            blocks = slice(first, first + count)
             nc.sync.dma_start(out=x_sb[:, blocks, :], in_=x_blocks[:, blocks, :])
 
-        load_x(0)
+        load_x(0, 2)
         for quad in range(4):
             nc.sync.dma_start(
                 out=w_scales[32 * quad : 32 * quad + 4, :].bitcast(I32),
                 in_=weight_scales[0, 4 * quad : 4 * quad + 4, :].bitcast(I32),
             )
         nc.sync.dma_start(out=w_words[:].bitcast(I32), in_=weight_words[0].bitcast(I32))
+        load_x(2, 2)
         for first in range(LOAD_BLOCKS, BLOCKS, LOAD_BLOCKS):
-            load_x(first)
+            load_x(first, LOAD_BLOCKS)
 
         x_codes = keep.tile([P, BLOCKS * P], U32, align_bytes=64)
         x_scales = keep.tile([P, BLOCKS * P], U8, align_bytes=64)
@@ -77,7 +79,7 @@ def tile_mylayerfunc_kernel(tc, x, weight_words, weight_scales, out):
                 for u in range(2):
                     nc.tensor.transpose(out=xt[:, i, u, :], in_=words[:, u:WORDS:2], identity=ident[:])
             grouped = stage.tile([P, 2 * P * 4], BF16, align_bytes=64)
-            nc.vector.tensor_copy(
+            nc.scalar.copy(
                 out=grouped[:].bitcast(F32).rearrange("p (i r u) -> p i r u", i=2, u=2),
                 in_=xt[:].rearrange("p i u r -> p i r u"),
             )
@@ -88,8 +90,9 @@ def tile_mylayerfunc_kernel(tc, x, weight_words, weight_scales, out):
 
         def one_block(m):
             planes = work.tile([P, 6, PER_BLOCK], F32)
-            half_sin = work.tile([P, 2, PER_BLOCK], F32)
+            abs_y = work.tile([P, 2, PER_BLOCK], F32)
             rows = slice(m * P, (m + 1) * P)
+            banks = []
             for h in range(HALVES):
                 y = psum_y.tile([P, BANK], F32)
                 nc.tensor.matmul_mx(
@@ -101,17 +104,17 @@ def tile_mylayerfunc_kernel(tc, x, weight_words, weight_scales, out):
                     start=True,
                     stop=True,
                 )
-                by_kind = y[:].rearrange("p (j c) -> p c j", c=KINDS)
-                js = slice(h * PER_BANK, (h + 1) * PER_BANK)
-                nc.scalar.activation(out=half_sin[:, :, js], in_=by_kind[:, COS : TAN + 1 : 2, :], func=ACT.Sin, scale=0.5)
-                nc.scalar.activation(out=planes[:, SIN : SIN_T + 1 : 3, js], in_=by_kind[:, SIN : TAN + 1, :], func=ACT.Sin)
-                nc.scalar.copy(out=planes[:, LIN, js], in_=by_kind[:, LIN, :])
-            nc.scalar.activation(out=half_sin[:], in_=half_sin[:], func=ACT.Square)
-            nc.vector.tensor_scalar(
-                out=planes[:, COS : COS_T + 1 : 3, :], in0=half_sin[:], scalar1=-2.0, scalar2=1.0, op0=ALU.mult, op1=ALU.add
+                banks.append((y[:].rearrange("p (j c) -> p c j", c=KINDS), slice(h * PER_BANK, (h + 1) * PER_BANK)))
+            for by_kind, js in banks:
+                nc.scalar.activation(out=abs_y[:, :, js], in_=by_kind[:, COS : TAN + 1 : 2, :], func=ACT.Abs)
+            nc.scalar.activation(
+                out=planes[:, COS : COS_T + 1 : 3, :], in_=abs_y[:], func=ACT.Sin, bias=math.pi / 2, scale=-1.0
             )
             inv_cos = work.tile([P, PER_BLOCK], F32)
             nc.vector.reciprocal(out=inv_cos[:], in_=planes[:, COS_T, :])
+            for by_kind, js in banks:
+                nc.scalar.activation(out=planes[:, SIN : SIN_T + 1 : 3, js], in_=by_kind[:, SIN : TAN + 1, :], func=ACT.Sin)
+                nc.scalar.copy(out=planes[:, LIN, js], in_=by_kind[:, LIN, :])
             nc.gpsimd.tensor_tensor(out=planes[:, TAN, :], in0=planes[:, SIN_T, :], in1=inv_cos[:], op=ALU.mult)
             woven = work.tile([P, N], F32)
             nc.gpsimd.tensor_scalar(

@@ -12,7 +12,6 @@ U8 = mybir.dt.uint8
 FP8X4 = mybir.dt.float8_e4m3fn_x4
 FP4X4 = mybir.dt.float4_e2m1fn_x4
 ACT = mybir.ActivationFunctionType
-ALU = mybir.AluOpType
 
 P = 128
 B, K, N = 2048, 512, 1024
@@ -21,7 +20,6 @@ BANK = 512
 HALVES = N // BANK
 KINDS = 4
 PER_BANK = BANK // KINDS
-PER_BLOCK = N // KINDS
 WORDS = K // 2
 LOAD_BLOCKS = 4
 
@@ -39,6 +37,7 @@ def tile_mylayerfunc_kernel(tc, x, weight_words, weight_scales, out):
         keep = ctx.enter_context(tc.tile_pool(name="keep", bufs=1))
         stage = ctx.enter_context(tc.tile_pool(name="stage", bufs=2))
         work = ctx.enter_context(tc.tile_pool(name="work", bufs=6))
+        small = ctx.enter_context(tc.tile_pool(name="small", bufs=4))
         psum_x = ctx.enter_context(tc.psum_pool(name="psum_x", bufs=2))
         psum_y = ctx.enter_context(tc.psum_pool(name="psum_y", bufs=6))
 
@@ -59,10 +58,10 @@ def tile_mylayerfunc_kernel(tc, x, weight_words, weight_scales, out):
             nc.sync.dma_start(out=x_sb[:, blocks, :], in_=x_blocks[:, blocks, :])
 
         load_x(0, 2)
-        for quad in range(4):
+        for quadrant in range(4):
             nc.sync.dma_start(
-                out=w_scales[32 * quad : 32 * quad + 4, :].bitcast(I32),
-                in_=weight_scales[0, 4 * quad : 4 * quad + 4, :].bitcast(I32),
+                out=w_scales[32 * quadrant : 32 * quadrant + 4, :].bitcast(I32),
+                in_=weight_scales[0, 4 * quadrant : 4 * quadrant + 4, :].bitcast(I32),
             )
         nc.sync.dma_start(out=w_words[:].bitcast(I32), in_=weight_words[0].bitcast(I32))
         load_x(2, 2)
@@ -72,7 +71,11 @@ def tile_mylayerfunc_kernel(tc, x, weight_words, weight_scales, out):
         x_codes = keep.tile([P, BLOCKS * P], U32, align_bytes=64)
         x_scales = keep.tile([P, BLOCKS * P], U8, align_bytes=64)
 
-        def quantise_two_blocks(first):
+        grouped_of = {}
+        planes_of = {}
+        pair_of, inv_quad_of, inv_pair_of, cross_of = {}, {}, {}, {}
+
+        def transpose_two_blocks(first):
             xt = psum_x.tile([P, 2, 2, P], F32)
             for i in range(2):
                 words = x_sb[:, first + i, :].bitcast(F32)
@@ -83,16 +86,19 @@ def tile_mylayerfunc_kernel(tc, x, weight_words, weight_scales, out):
                 out=grouped[:].bitcast(F32).rearrange("p (i r u) -> p i r u", i=2, u=2),
                 in_=xt[:].rearrange("p i u r -> p i r u"),
             )
+            grouped_of[first] = grouped
+
+        def quantise_two_blocks(first):
             cols = slice(first * P, (first + 2) * P)
             nc.vector.quantize_mx(
-                out=x_codes[:, cols].bitcast(FP8X4), scales=x_scales[:, cols], in_=grouped[:]
+                out=x_codes[:, cols].bitcast(FP8X4), scales=x_scales[:, cols], in_=grouped_of[first][:]
             )
 
-        def one_block(m):
-            planes = work.tile([P, 6, PER_BLOCK], F32)
-            abs_y = work.tile([P, 2, PER_BLOCK], F32)
+        def multiply_and_functions(m):
+            planes = work.tile([P, 6, HALVES, PER_BANK], F32)
+            abs_y = work.tile([P, 2, HALVES, PER_BANK], F32)
             rows = slice(m * P, (m + 1) * P)
-            banks = []
+            by_kind = []
             for h in range(HALVES):
                 y = psum_y.tile([P, BANK], F32)
                 nc.tensor.matmul_mx(
@@ -104,32 +110,73 @@ def tile_mylayerfunc_kernel(tc, x, weight_words, weight_scales, out):
                     start=True,
                     stop=True,
                 )
-                banks.append((y[:].rearrange("p (j c) -> p c j", c=KINDS), slice(h * PER_BANK, (h + 1) * PER_BANK)))
-            for by_kind, js in banks:
-                nc.scalar.activation(out=abs_y[:, :, js], in_=by_kind[:, COS : TAN + 1 : 2, :], func=ACT.Abs)
+                by_kind.append(y[:].rearrange("p (j c) -> p c j", c=KINDS))
+            for h in range(HALVES):
+                nc.scalar.activation(out=abs_y[:, :, h, :], in_=by_kind[h][:, COS : TAN + 1 : 2, :], func=ACT.Abs)
             nc.scalar.activation(
-                out=planes[:, COS : COS_T + 1 : 3, :], in_=abs_y[:], func=ACT.Sin, bias=math.pi / 2, scale=-1.0
+                out=planes[:, COS : COS_T + 1 : 3, :, :], in_=abs_y[:], func=ACT.Sin, bias=math.pi / 2, scale=-1.0
             )
-            inv_cos = work.tile([P, PER_BLOCK], F32)
-            nc.vector.reciprocal(out=inv_cos[:], in_=planes[:, COS_T, :])
-            for by_kind, js in banks:
-                nc.scalar.activation(out=planes[:, SIN : SIN_T + 1 : 3, js], in_=by_kind[:, SIN : TAN + 1, :], func=ACT.Sin)
-                nc.scalar.copy(out=planes[:, LIN, js], in_=by_kind[:, LIN, :])
-            nc.gpsimd.tensor_tensor(out=planes[:, TAN, :], in0=planes[:, SIN_T, :], in1=inv_cos[:], op=ALU.mult)
+            for h in range(HALVES):
+                nc.scalar.activation(out=planes[:, SIN : SIN_T + 1 : 3, h, :], in_=by_kind[h][:, SIN : TAN + 1, :], func=ACT.Sin)
+                nc.scalar.copy(out=planes[:, LIN, h, :], in_=by_kind[h][:, LIN, :])
+            planes_of[m] = planes
+
+        def products_up(m):
+            planes = planes_of[m]
+            pair = small.tile([P, 2, PER_BANK // 2], F32)
+            nc.vector.tensor_mul(
+                out=pair[:].rearrange("p q i -> p (q i)"), in0=planes[:, COS_T, 0, :], in1=planes[:, COS_T, 1, :]
+            )
+            pair_of[m] = pair
+
+        def quad_and_cross_and_reciprocal(m):
+            planes, pair = planes_of[m], pair_of[m]
+            quad = small.tile([P, PER_BANK // 2], F32)
+            nc.vector.tensor_mul(out=quad[:], in0=pair[:, 0, :], in1=pair[:, 1, :])
+            cross = small.tile([P, HALVES, PER_BANK], F32)
+            for h in range(HALVES):
+                nc.vector.tensor_mul(out=cross[:, h, :], in0=planes[:, SIN_T, h, :], in1=planes[:, COS_T, 1 - h, :])
+            inv_quad = small.tile([P, PER_BANK // 2], F32)
+            nc.vector.reciprocal(out=inv_quad[:], in_=quad[:])
+            cross_of[m], inv_quad_of[m] = cross, inv_quad
+
+        def products_down(m):
+            inv_pair = small.tile([P, 2, PER_BANK // 2], F32)
+            for q in range(2):
+                nc.vector.tensor_mul(out=inv_pair[:, q, :], in0=inv_quad_of[m][:], in1=pair_of[m][:, 1 - q, :])
+            inv_pair_of[m] = inv_pair
+
+        def tangent(m):
+            nc.vector.tensor_mul(
+                out=planes_of[m][:, TAN, :, :],
+                in0=cross_of[m][:],
+                in1=inv_pair_of[m][:].rearrange("p q i -> p (q i)").unsqueeze(1).to_broadcast([P, HALVES, PER_BANK]),
+            )
+
+        def weave_and_store(m):
             woven = work.tile([P, N], F32)
-            nc.gpsimd.tensor_scalar(
-                out=woven[:].rearrange("p (j c) -> p j c", c=KINDS),
-                in0=planes[:, LIN : TAN + 1, :].rearrange("p c j -> p j c"),
-                scalar1=1.0,
-                scalar2=0.0,
-                op0=ALU.mult,
-                op1=ALU.add,
+            nc.vector.tensor_copy(
+                out=woven[:].rearrange("p (n c) -> p n c", c=KINDS),
+                in_=planes_of[m][:, LIN : TAN + 1, :, :].rearrange("p c h j -> p (h j) c"),
             )
             nc.sync.dma_start(out=out_blocks[:, m, :], in_=woven[:])
 
+        transpose_two_blocks(0)
         quantise_two_blocks(0)
-        for first in range(0, BLOCKS, 2):
-            if first + 2 < BLOCKS:
-                quantise_two_blocks(first + 2)
-            one_block(first)
-            one_block(first + 1)
+        for m in range(BLOCKS + 2):
+            more_x = 2 * m + 2 < BLOCKS
+            if m < BLOCKS:
+                multiply_and_functions(m)
+                if more_x:
+                    transpose_two_blocks(2 * m + 2)
+                products_up(m)
+            if 1 <= m <= BLOCKS:
+                products_down(m - 1)
+            if m < BLOCKS:
+                quad_and_cross_and_reciprocal(m)
+            if 1 <= m <= BLOCKS:
+                tangent(m - 1)
+            if m >= 2:
+                weave_and_store(m - 2)
+            if more_x:
+                quantise_two_blocks(2 * m + 2)

@@ -12,6 +12,7 @@ U8 = mybir.dt.uint8
 FP8X4 = mybir.dt.float8_e4m3fn_x4
 FP4X4 = mybir.dt.float4_e2m1fn_x4
 ACT = mybir.ActivationFunctionType
+ALU = mybir.AluOpType
 
 P = 128
 B, K, N = 2048, 512, 1024
@@ -22,6 +23,7 @@ KINDS = 4
 PER_BANK = BANK // KINDS
 WORDS = K // 2
 LOAD_BLOCKS = 4
+UNITS = BLOCKS // 2
 
 LIN, COS, SIN, TAN, COS_T, SIN_T = 0, 1, 2, 3, 4, 5
 
@@ -36,8 +38,8 @@ def tile_mylayerfunc_kernel(tc, x, weight_words, weight_scales, out):
     with ExitStack() as ctx:
         keep = ctx.enter_context(tc.tile_pool(name="keep", bufs=1))
         stage = ctx.enter_context(tc.tile_pool(name="stage", bufs=2))
-        work = ctx.enter_context(tc.tile_pool(name="work", bufs=6))
-        small = ctx.enter_context(tc.tile_pool(name="small", bufs=4))
+        work = ctx.enter_context(tc.tile_pool(name="work", bufs=4))
+        small = ctx.enter_context(tc.tile_pool(name="small", bufs=3))
         psum_x = ctx.enter_context(tc.psum_pool(name="psum_x", bufs=2))
         psum_y = ctx.enter_context(tc.psum_pool(name="psum_y", bufs=6))
 
@@ -75,108 +77,111 @@ def tile_mylayerfunc_kernel(tc, x, weight_words, weight_scales, out):
         planes_of = {}
         pair_of, inv_quad_of, inv_pair_of, cross_of = {}, {}, {}, {}
 
-        def transpose_two_blocks(first):
+        def transpose_x(u):
             xt = psum_x.tile([P, 2, 2, P], F32)
             for i in range(2):
-                words = x_sb[:, first + i, :].bitcast(F32)
-                for u in range(2):
-                    nc.tensor.transpose(out=xt[:, i, u, :], in_=words[:, u:WORDS:2], identity=ident[:])
+                words = x_sb[:, 2 * u + i, :].bitcast(F32)
+                for u2 in range(2):
+                    nc.tensor.transpose(out=xt[:, i, u2, :], in_=words[:, u2:WORDS:2], identity=ident[:])
             grouped = stage.tile([P, 2 * P * 4], BF16, align_bytes=64)
             nc.scalar.copy(
-                out=grouped[:].bitcast(F32).rearrange("p (i r u) -> p i r u", i=2, u=2),
-                in_=xt[:].rearrange("p i u r -> p i r u"),
+                out=grouped[:].bitcast(F32).rearrange("p (i r u2) -> p i r u2", i=2, u2=2),
+                in_=xt[:].rearrange("p i u2 r -> p i r u2"),
             )
-            grouped_of[first] = grouped
+            grouped_of[u] = grouped
 
-        def quantise_two_blocks(first):
-            cols = slice(first * P, (first + 2) * P)
+        def quantise_x(u):
+            cols = slice(2 * u * P, (2 * u + 2) * P)
             nc.vector.quantize_mx(
-                out=x_codes[:, cols].bitcast(FP8X4), scales=x_scales[:, cols], in_=grouped_of[first][:]
+                out=x_codes[:, cols].bitcast(FP8X4), scales=x_scales[:, cols], in_=grouped_of[u][:]
             )
 
-        def multiply_and_functions(m):
-            planes = work.tile([P, 6, HALVES, PER_BANK], F32)
-            abs_y = work.tile([P, 2, HALVES, PER_BANK], F32)
-            rows = slice(m * P, (m + 1) * P)
-            by_kind = []
-            for h in range(HALVES):
-                y = psum_y.tile([P, BANK], F32)
-                nc.tensor.matmul_mx(
-                    out=y[:],
-                    lhsT=x_codes[:, rows].bitcast(FP8X4),
-                    lhsT_scale=x_scales[:, rows],
-                    rhs=w_words[:, 2 * BANK * h : 2 * BANK * (h + 1)].bitcast(FP4X4),
-                    rhs_scale=w_scales[:, BANK * h : BANK * (h + 1)],
-                    start=True,
-                    stop=True,
-                )
-                by_kind.append(y[:].rearrange("p (j c) -> p c j", c=KINDS))
-            for h in range(HALVES):
-                nc.scalar.activation(out=abs_y[:, :, h, :], in_=by_kind[h][:, COS : TAN + 1 : 2, :], func=ACT.Abs)
+        def multiply_and_functions(u):
+            planes = work.tile([P, 6, 2, HALVES, PER_BANK], F32)
+            abs_y = work.tile([P, 2, 2, HALVES, PER_BANK], F32)
+            banks = []
+            for i in range(2):
+                rows = slice((2 * u + i) * P, (2 * u + i + 1) * P)
+                for h in range(HALVES):
+                    y = psum_y.tile([P, BANK], F32)
+                    nc.tensor.matmul_mx(
+                        out=y[:],
+                        lhsT=x_codes[:, rows].bitcast(FP8X4),
+                        lhsT_scale=x_scales[:, rows],
+                        rhs=w_words[:, 2 * BANK * h : 2 * BANK * (h + 1)].bitcast(FP4X4),
+                        rhs_scale=w_scales[:, BANK * h : BANK * (h + 1)],
+                        start=True,
+                        stop=True,
+                    )
+                    banks.append((i, h, y[:].rearrange("p (j c) -> p c j", c=KINDS)))
+            for i, h, by_kind in banks:
+                nc.scalar.activation(out=abs_y[:, :, i, h, :], in_=by_kind[:, COS : TAN + 1 : 2, :], func=ACT.Abs)
             nc.scalar.activation(
-                out=planes[:, COS : COS_T + 1 : 3, :, :], in_=abs_y[:], func=ACT.Sin, bias=math.pi / 2, scale=-1.0
+                out=planes[:, COS : COS_T + 1 : 3, :, :, :], in_=abs_y[:], func=ACT.Sin, bias=math.pi / 2, scale=-1.0
             )
-            for h in range(HALVES):
-                nc.scalar.activation(out=planes[:, SIN : SIN_T + 1 : 3, h, :], in_=by_kind[h][:, SIN : TAN + 1, :], func=ACT.Sin)
-                nc.scalar.copy(out=planes[:, LIN, h, :], in_=by_kind[h][:, LIN, :])
-            planes_of[m] = planes
+            for i, h, by_kind in banks:
+                nc.scalar.activation(out=planes[:, SIN : SIN_T + 1 : 3, i, h, :], in_=by_kind[:, SIN : TAN + 1, :], func=ACT.Sin)
+                nc.scalar.copy(out=planes[:, LIN, i, h, :], in_=by_kind[:, LIN, :])
+            planes_of[u] = planes
 
-        def products_up(m):
-            planes = planes_of[m]
-            pair = small.tile([P, 2, PER_BANK // 2], F32)
-            nc.vector.tensor_mul(
-                out=pair[:].rearrange("p q i -> p (q i)"), in0=planes[:, COS_T, 0, :], in1=planes[:, COS_T, 1, :]
-            )
-            pair_of[m] = pair
+        def products_up(u):
+            planes = planes_of[u]
+            pair = small.tile([P, 2, PER_BANK], F32)
+            nc.vector.tensor_mul(out=pair[:], in0=planes[:, COS_T, :, 0, :], in1=planes[:, COS_T, :, 1, :])
+            pair_of[u] = pair
 
-        def quad_and_cross_and_reciprocal(m):
-            planes, pair = planes_of[m], pair_of[m]
-            quad = small.tile([P, PER_BANK // 2], F32)
+        def quad_and_cross_and_reciprocal(u):
+            planes, pair = planes_of[u], pair_of[u]
+            quad = small.tile([P, PER_BANK], F32)
             nc.vector.tensor_mul(out=quad[:], in0=pair[:, 0, :], in1=pair[:, 1, :])
-            cross = small.tile([P, HALVES, PER_BANK], F32)
+            cross = small.tile([P, 2, HALVES, PER_BANK], F32)
             for h in range(HALVES):
-                nc.vector.tensor_mul(out=cross[:, h, :], in0=planes[:, SIN_T, h, :], in1=planes[:, COS_T, 1 - h, :])
-            inv_quad = small.tile([P, PER_BANK // 2], F32)
+                nc.vector.tensor_mul(out=cross[:, :, h, :], in0=planes[:, SIN_T, :, h, :], in1=planes[:, COS_T, :, 1 - h, :])
+            inv_quad = small.tile([P, PER_BANK], F32)
             nc.vector.reciprocal(out=inv_quad[:], in_=quad[:])
-            cross_of[m], inv_quad_of[m] = cross, inv_quad
+            cross_of[u], inv_quad_of[u] = cross, inv_quad
 
-        def products_down(m):
-            inv_pair = small.tile([P, 2, PER_BANK // 2], F32)
-            for q in range(2):
-                nc.vector.tensor_mul(out=inv_pair[:, q, :], in0=inv_quad_of[m][:], in1=pair_of[m][:, 1 - q, :])
-            inv_pair_of[m] = inv_pair
+        def products_down(u):
+            inv_pair = small.tile([P, 2, PER_BANK], F32)
+            for i in range(2):
+                nc.vector.tensor_mul(out=inv_pair[:, i, :], in0=inv_quad_of[u][:], in1=pair_of[u][:, 1 - i, :])
+            inv_pair_of[u] = inv_pair
 
-        def tangent(m):
+        def tangent(u):
             nc.vector.tensor_mul(
-                out=planes_of[m][:, TAN, :, :],
-                in0=cross_of[m][:],
-                in1=inv_pair_of[m][:].rearrange("p q i -> p (q i)").unsqueeze(1).to_broadcast([P, HALVES, PER_BANK]),
+                out=planes_of[u][:, TAN, :, :, :],
+                in0=cross_of[u][:],
+                in1=inv_pair_of[u][:].unsqueeze(2).to_broadcast([P, 2, HALVES, PER_BANK]),
             )
 
-        def weave_and_store(m):
-            woven = work.tile([P, N], F32)
-            nc.vector.tensor_copy(
-                out=woven[:].rearrange("p (n c) -> p n c", c=KINDS),
-                in_=planes_of[m][:, LIN : TAN + 1, :, :].rearrange("p c h j -> p (h j) c"),
-            )
-            nc.sync.dma_start(out=out_blocks[:, m, :], in_=woven[:])
+        def weave_and_store(u):
+            for i in range(2):
+                woven = work.tile([P, N], F32, name="woven%d" % i)
+                woven_view = woven[:].rearrange("p (n c) -> p n c", c=KINDS)
+                planes_view = planes_of[u][:, LIN : TAN + 1, i, :, :].rearrange("p c h j -> p (h j) c")
+                if i == 0:
+                    nc.vector.tensor_copy(out=woven_view, in_=planes_view)
+                else:
+                    nc.gpsimd.tensor_scalar(
+                        out=woven_view, in0=planes_view, scalar1=1.0, scalar2=0.0, op0=ALU.mult, op1=ALU.add
+                    )
+                nc.sync.dma_start(out=out_blocks[:, 2 * u + i, :], in_=woven[:])
 
-        transpose_two_blocks(0)
-        quantise_two_blocks(0)
-        for m in range(BLOCKS + 2):
-            more_x = 2 * m + 2 < BLOCKS
-            if m < BLOCKS:
-                multiply_and_functions(m)
-                if more_x:
-                    transpose_two_blocks(2 * m + 2)
-                products_up(m)
-            if 1 <= m <= BLOCKS:
-                products_down(m - 1)
-            if m < BLOCKS:
-                quad_and_cross_and_reciprocal(m)
-            if 1 <= m <= BLOCKS:
-                tangent(m - 1)
-            if m >= 2:
-                weave_and_store(m - 2)
-            if more_x:
-                quantise_two_blocks(2 * m + 2)
+        transpose_x(0)
+        quantise_x(0)
+        for u in range(UNITS + 2):
+            if u < UNITS:
+                multiply_and_functions(u)
+                if u + 1 < UNITS:
+                    transpose_x(u + 1)
+                products_up(u)
+            if 1 <= u <= UNITS:
+                products_down(u - 1)
+            if u < UNITS:
+                quad_and_cross_and_reciprocal(u)
+            if 1 <= u <= UNITS:
+                tangent(u - 1)
+            if u >= 2:
+                weave_and_store(u - 2)
+            if u + 1 < UNITS:
+                quantise_x(u + 1)

@@ -12,7 +12,6 @@ U8 = mybir.dt.uint8
 FP8X4 = mybir.dt.float8_e4m3fn_x4
 FP4X4 = mybir.dt.float4_e2m1fn_x4
 ACT = mybir.ActivationFunctionType
-ALU = mybir.AluOpType
 
 P = 128
 B, K, N = 2048, 512, 1024
@@ -23,7 +22,6 @@ KINDS = 4
 PER_BANK = BANK // KINDS
 WORDS = K // 2
 LOAD_BLOCKS = 4
-UNITS = BLOCKS // 2
 
 LIN, COS, SIN, TAN, COS_T, SIN_T = 0, 1, 2, 3, 4, 5
 
@@ -36,10 +34,11 @@ def tile_mylayerfunc_kernel(tc, x, weight_words, weight_scales, out):
     out_blocks = out.rearrange("(p m) n -> p m n", m=BLOCKS)
 
     with ExitStack() as ctx:
+        ctx.enter_context(tc.manual_schedule())
         keep = ctx.enter_context(tc.tile_pool(name="keep", bufs=1))
         stage = ctx.enter_context(tc.tile_pool(name="stage", bufs=2))
-        work = ctx.enter_context(tc.tile_pool(name="work", bufs=4))
-        small = ctx.enter_context(tc.tile_pool(name="small", bufs=3))
+        work = ctx.enter_context(tc.tile_pool(name="work", bufs=6))
+        small = ctx.enter_context(tc.tile_pool(name="small", bufs=4))
         psum_x = ctx.enter_context(tc.psum_pool(name="psum_x", bufs=2))
         psum_y = ctx.enter_context(tc.psum_pool(name="psum_y", bufs=6))
 
@@ -75,113 +74,127 @@ def tile_mylayerfunc_kernel(tc, x, weight_words, weight_scales, out):
 
         grouped_of = {}
         planes_of = {}
-        pair_of, inv_quad_of, inv_pair_of, cross_of = {}, {}, {}, {}
+        pair_of, quad_of, inv_quad_of, inv_pair_of, cross_of = {}, {}, {}, {}, {}
 
-        def transpose_x(u):
+        def transpose_two_blocks(first):
             xt = psum_x.tile([P, 2, 2, P], F32)
             for i in range(2):
-                words = x_sb[:, 2 * u + i, :].bitcast(F32)
-                for u2 in range(2):
-                    nc.tensor.transpose(out=xt[:, i, u2, :], in_=words[:, u2:WORDS:2], identity=ident[:])
+                words = x_sb[:, first + i, :].bitcast(F32)
+                for u in range(2):
+                    nc.tensor.transpose(out=xt[:, i, u, :], in_=words[:, u:WORDS:2], identity=ident[:])
             grouped = stage.tile([P, 2 * P * 4], BF16, align_bytes=64)
             nc.scalar.copy(
-                out=grouped[:].bitcast(F32).rearrange("p (i r u2) -> p i r u2", i=2, u2=2),
-                in_=xt[:].rearrange("p i u2 r -> p i r u2"),
+                out=grouped[:].bitcast(F32).rearrange("p (i r u) -> p i r u", i=2, u=2),
+                in_=xt[:].rearrange("p i u r -> p i r u"),
             )
-            grouped_of[u] = grouped
+            grouped_of[first] = grouped
 
-        def quantise_x(u):
-            cols = slice(2 * u * P, (2 * u + 2) * P)
+        def quantise_two_blocks(first):
+            cols = slice(first * P, (first + 2) * P)
             nc.vector.quantize_mx(
-                out=x_codes[:, cols].bitcast(FP8X4), scales=x_scales[:, cols], in_=grouped_of[u][:]
+                out=x_codes[:, cols].bitcast(FP8X4), scales=x_scales[:, cols], in_=grouped_of[first][:]
             )
 
-        def multiply_and_functions(u):
-            planes = work.tile([P, 6, 2, HALVES, PER_BANK], F32)
-            abs_y = work.tile([P, 2, 2, HALVES, PER_BANK], F32)
-            banks = []
-            for i in range(2):
-                rows = slice((2 * u + i) * P, (2 * u + i + 1) * P)
-                for h in range(HALVES):
-                    y = psum_y.tile([P, BANK], F32)
-                    nc.tensor.matmul_mx(
-                        out=y[:],
-                        lhsT=x_codes[:, rows].bitcast(FP8X4),
-                        lhsT_scale=x_scales[:, rows],
-                        rhs=w_words[:, 2 * BANK * h : 2 * BANK * (h + 1)].bitcast(FP4X4),
-                        rhs_scale=w_scales[:, BANK * h : BANK * (h + 1)],
-                        start=True,
-                        stop=True,
-                    )
-                    banks.append((i, h, y[:].rearrange("p (j c) -> p c j", c=KINDS)))
-            for i, h, by_kind in banks:
-                nc.scalar.activation(out=abs_y[:, :, i, h, :], in_=by_kind[:, COS : TAN + 1 : 2, :], func=ACT.Abs)
-            nc.scalar.activation(
-                out=planes[:, COS : COS_T + 1 : 3, :, :, :], in_=abs_y[:], func=ACT.Sin, bias=math.pi / 2, scale=-1.0
-            )
-            for i, h, by_kind in banks:
-                nc.scalar.activation(out=planes[:, SIN : SIN_T + 1 : 3, i, h, :], in_=by_kind[:, SIN : TAN + 1, :], func=ACT.Sin)
-                nc.scalar.copy(out=planes[:, LIN, i, h, :], in_=by_kind[:, LIN, :])
-            planes_of[u] = planes
-
-        def products_up(u):
-            planes = planes_of[u]
-            pair = small.tile([P, 2, PER_BANK], F32)
-            nc.vector.tensor_mul(out=pair[:], in0=planes[:, COS_T, :, 0, :], in1=planes[:, COS_T, :, 1, :])
-            pair_of[u] = pair
-
-        def quad_and_cross_and_reciprocal(u):
-            planes, pair = planes_of[u], pair_of[u]
-            quad = small.tile([P, PER_BANK], F32)
-            nc.vector.tensor_mul(out=quad[:], in0=pair[:, 0, :], in1=pair[:, 1, :])
-            cross = small.tile([P, 2, HALVES, PER_BANK], F32)
+        def multiply_and_functions(m):
+            planes = work.tile([P, 6, HALVES, PER_BANK], F32)
+            abs_y = work.tile([P, 2, HALVES, PER_BANK], F32)
+            rows = slice(m * P, (m + 1) * P)
+            by_kind = []
             for h in range(HALVES):
-                nc.vector.tensor_mul(out=cross[:, :, h, :], in0=planes[:, SIN_T, :, h, :], in1=planes[:, COS_T, :, 1 - h, :])
-            inv_quad = small.tile([P, PER_BANK], F32)
-            nc.vector.reciprocal(out=inv_quad[:], in_=quad[:])
-            cross_of[u], inv_quad_of[u] = cross, inv_quad
+                y = psum_y.tile([P, BANK], F32)
+                nc.tensor.matmul_mx(
+                    out=y[:],
+                    lhsT=x_codes[:, rows].bitcast(FP8X4),
+                    lhsT_scale=x_scales[:, rows],
+                    rhs=w_words[:, 2 * BANK * h : 2 * BANK * (h + 1)].bitcast(FP4X4),
+                    rhs_scale=w_scales[:, BANK * h : BANK * (h + 1)],
+                    start=True,
+                    stop=True,
+                )
+                by_kind.append(y[:].rearrange("p (j c) -> p c j", c=KINDS))
+            def sines(h):
+                nc.scalar.activation(out=planes[:, SIN : SIN_T + 1 : 3, h, :], in_=by_kind[h][:, SIN : TAN + 1, :], func=ACT.Sin)
 
-        def products_down(u):
-            inv_pair = small.tile([P, 2, PER_BANK], F32)
-            for i in range(2):
-                nc.vector.tensor_mul(out=inv_pair[:, i, :], in0=inv_quad_of[u][:], in1=pair_of[u][:, 1 - i, :])
-            inv_pair_of[u] = inv_pair
+            for h in range(HALVES):
+                nc.scalar.activation(out=abs_y[:, :, h, :], in_=by_kind[h][:, COS : TAN + 1 : 2, :], func=ACT.Abs)
+            sines(0)
+            nc.scalar.activation(
+                out=planes[:, COS : COS_T + 1 : 3, :, :], in_=abs_y[:], func=ACT.Sin, bias=math.pi / 2, scale=-1.0
+            )
+            sines(1)
+            for h in range(HALVES):
+                nc.scalar.copy(out=planes[:, LIN, h, :], in_=by_kind[h][:, LIN, :])
+            planes_of[m] = planes
 
-        def tangent(u):
+        def products_up(m):
+            planes = planes_of[m]
+            pair = small.tile([P, 2, PER_BANK // 2], F32)
             nc.vector.tensor_mul(
-                out=planes_of[u][:, TAN, :, :, :],
-                in0=cross_of[u][:],
-                in1=inv_pair_of[u][:].unsqueeze(2).to_broadcast([P, 2, HALVES, PER_BANK]),
+                out=pair[:].rearrange("p q i -> p (q i)"), in0=planes[:, COS_T, 0, :], in1=planes[:, COS_T, 1, :]
+            )
+            pair_of[m] = pair
+
+        def product_of_four(m):
+            pair = pair_of[m]
+            quad = small.tile([P, PER_BANK // 2], F32)
+            nc.vector.tensor_mul(out=quad[:], in0=pair[:, 0, :], in1=pair[:, 1, :])
+            quad_of[m] = quad
+
+        def reciprocal(m):
+            inv_quad = small.tile([P, PER_BANK // 2], F32)
+            nc.vector.reciprocal(out=inv_quad[:], in_=quad_of[m][:])
+            inv_quad_of[m] = inv_quad
+
+        def cross_product(m, h):
+            planes = planes_of[m]
+            if h == 0:
+                cross_of[m] = small.tile([P, HALVES, PER_BANK], F32, name="cross")
+            nc.vector.tensor_mul(out=cross_of[m][:, h, :], in0=planes[:, SIN_T, h, :], in1=planes[:, COS_T, 1 - h, :])
+
+        def products_down(m):
+            inv_pair = small.tile([P, 2, PER_BANK // 2], F32)
+            for q in range(2):
+                nc.vector.tensor_mul(out=inv_pair[:, q, :], in0=inv_quad_of[m][:], in1=pair_of[m][:, 1 - q, :])
+            inv_pair_of[m] = inv_pair
+
+        def tangent(m):
+            nc.vector.tensor_mul(
+                out=planes_of[m][:, TAN, :, :],
+                in0=cross_of[m][:],
+                in1=inv_pair_of[m][:].rearrange("p q i -> p (q i)").unsqueeze(1).to_broadcast([P, HALVES, PER_BANK]),
             )
 
-        def weave_and_store(u):
-            for i in range(2):
-                woven = work.tile([P, N], F32, name="woven%d" % i)
-                woven_view = woven[:].rearrange("p (n c) -> p n c", c=KINDS)
-                planes_view = planes_of[u][:, LIN : TAN + 1, i, :, :].rearrange("p c h j -> p (h j) c")
-                if i == 0:
-                    nc.vector.tensor_copy(out=woven_view, in_=planes_view)
-                else:
-                    nc.gpsimd.tensor_scalar(
-                        out=woven_view, in0=planes_view, scalar1=1.0, scalar2=0.0, op0=ALU.mult, op1=ALU.add
-                    )
-                nc.sync.dma_start(out=out_blocks[:, 2 * u + i, :], in_=woven[:])
+        def weave_and_store(m, h):
+            woven = work.tile([P, BANK], F32)
+            nc.vector.tensor_copy(
+                out=woven[:].rearrange("p (j c) -> p j c", c=KINDS),
+                in_=planes_of[m][:, LIN : TAN + 1, h, :].rearrange("p c j -> p j c"),
+            )
+            nc.sync.dma_start(out=out_blocks[:, m, BANK * h : BANK * (h + 1)], in_=woven[:])
 
-        transpose_x(0)
-        quantise_x(0)
-        for u in range(UNITS + 2):
-            if u < UNITS:
-                multiply_and_functions(u)
-                if u + 1 < UNITS:
-                    transpose_x(u + 1)
-                products_up(u)
-            if 1 <= u <= UNITS:
-                products_down(u - 1)
-            if u < UNITS:
-                quad_and_cross_and_reciprocal(u)
-            if 1 <= u <= UNITS:
-                tangent(u - 1)
-            if u >= 2:
-                weave_and_store(u - 2)
-            if u + 1 < UNITS:
-                quantise_x(u + 1)
+        transpose_two_blocks(0)
+        quantise_two_blocks(0)
+        for m in range(BLOCKS + 2):
+            more_x = 2 * m + 2 < BLOCKS
+            going_up, going_down, weaving = m < BLOCKS, 1 <= m <= BLOCKS, m >= 2
+            if going_up:
+                multiply_and_functions(m)
+                if more_x:
+                    transpose_two_blocks(2 * m + 2)
+            if weaving:
+                weave_and_store(m - 2, 0)
+            if going_down:
+                products_down(m - 1)
+            if weaving:
+                weave_and_store(m - 2, 1)
+            if going_up:
+                products_up(m)
+            if going_down:
+                tangent(m - 1)
+            if going_up:
+                product_of_four(m)
+                cross_product(m, 0)
+                cross_product(m, 1)
+                reciprocal(m)
+            if more_x:
+                quantise_two_blocks(2 * m + 2)

@@ -97,7 +97,7 @@ def tile_mylayerfunc_kernel(tc, x, weight_words, weight_scales, out):
 
         def multiply_and_functions(m):
             planes = work.tile([P, 6, HALVES, PER_BANK], F32)
-            abs_y = work.tile([P, 2, HALVES, PER_BANK], F32)
+            abs_y = work.tile([P, 2 * HALVES, PER_BANK], F32)
             rows = slice(m * P, (m + 1) * P)
             by_kind = []
             for h in range(HALVES):
@@ -115,11 +115,13 @@ def tile_mylayerfunc_kernel(tc, x, weight_words, weight_scales, out):
             def sines(h):
                 nc.scalar.activation(out=planes[:, SIN : SIN_T + 1 : 3, h, :], in_=by_kind[h][:, SIN : TAN + 1, :], func=ACT.Sin)
 
-            for h in range(HALVES):
-                nc.scalar.activation(out=abs_y[:, :, h, :], in_=by_kind[h][:, COS : TAN + 1 : 2, :], func=ACT.Abs)
+            nc.scalar.activation(out=abs_y[:, 0:4:3, :], in_=by_kind[0][:, COS : TAN + 1 : 2, :], func=ACT.Abs)
+            nc.scalar.activation(out=abs_y[:, 1:3, :], in_=by_kind[1][:, COS : TAN + 1 : 2, :], func=ACT.Abs)
             sines(0)
             nc.scalar.activation(
-                out=planes[:, COS : COS_T + 1 : 3, :, :], in_=abs_y[:], func=ACT.Sin, bias=math.pi / 2, scale=-1.0
+                out=planes[:, COS : COS_T + 1 : 3, :, :],
+                in_=abs_y[:].rearrange("p (c h) j -> p c h j", h=HALVES),
+                func=ACT.Sin, bias=math.pi / 2, scale=-1.0
             )
             sines(1)
             for h in range(HALVES):
@@ -145,16 +147,19 @@ def tile_mylayerfunc_kernel(tc, x, weight_words, weight_scales, out):
             nc.vector.reciprocal(out=inv_quad[:], in_=quad_of[m][:])
             inv_quad_of[m] = inv_quad
 
-        def cross_product(m, h):
+        def cross_product(m):
             planes = planes_of[m]
-            if h == 0:
-                cross_of[m] = small.tile([P, HALVES, PER_BANK], F32, name="cross")
-            nc.vector.tensor_mul(out=cross_of[m][:, h, :], in0=planes[:, SIN_T, h, :], in1=planes[:, COS_T, 1 - h, :])
+            cross = small.tile([P, HALVES, PER_BANK], F32)
+            nc.vector.tensor_mul(out=cross[:], in0=planes[:, SIN_T, :, :], in1=planes[:, COS_T, :, :])
+            cross_of[m] = cross
 
         def products_down(m):
             inv_pair = small.tile([P, 2, PER_BANK // 2], F32)
-            for q in range(2):
-                nc.vector.tensor_mul(out=inv_pair[:, q, :], in0=inv_quad_of[m][:], in1=pair_of[m][:, 1 - q, :])
+            nc.vector.tensor_mul(
+                out=inv_pair[:],
+                in0=inv_quad_of[m][:].unsqueeze(1).to_broadcast([P, 2, PER_BANK // 2]),
+                in1=pair_of[m][:, ::-1, :],
+            )
             inv_pair_of[m] = inv_pair
 
         def tangent(m):
@@ -193,8 +198,7 @@ def tile_mylayerfunc_kernel(tc, x, weight_words, weight_scales, out):
                 tangent(m - 1)
             if going_up:
                 product_of_four(m)
-                cross_product(m, 0)
-                cross_product(m, 1)
+                cross_product(m)
                 reciprocal(m)
             if more_x:
                 quantise_two_blocks(2 * m + 2)

@@ -17,11 +17,13 @@ P = 128
 B, K, N = 2048, 512, 1024
 BLOCKS = B // P
 BANK = 512
-HALVES = N // BANK
 KINDS = 4
-PER_BANK = BANK // KINDS
+GROUPS = N // KINDS
+HALF = GROUPS // 2
+QUARTER = GROUPS // 4
 WORDS = K // 2
 LOAD_BLOCKS = 4
+VECTOR_COPIES_UP_TO = 6
 
 LIN, COS, SIN, TAN, COS_T, SIN_T = 0, 1, 2, 3, 4, 5
 
@@ -46,13 +48,13 @@ def tile_mylayerfunc_kernel(tc, x, weight_words, weight_scales, out):
         nc.vector.memset(table_warm[:], 0.0)
         nc.scalar.activation(out=table_warm[:], in_=table_warm[:], func=ACT.Sin)
 
-        w_scales = keep.tile([P, N], U8, align_bytes=64)
-        nc.vector.memset(w_scales[:].bitcast(I32), 0)
+        scales_in = keep.tile([P, N], U8, align_bytes=64)
+        nc.vector.memset(scales_in[:].bitcast(I32), 0)
         ident = keep.tile([P, P], F32)
         make_identity(nc, ident[:])
 
         x_sb = keep.tile([P, BLOCKS, K], BF16)
-        w_words = keep.tile([P, 2 * N], U8, align_bytes=64)
+        words_in = keep.tile([P, 2 * N], U8, align_bytes=64)
 
         def load_x(first, count):
             blocks = slice(first, first + count)
@@ -61,13 +63,24 @@ def tile_mylayerfunc_kernel(tc, x, weight_words, weight_scales, out):
         load_x(0, 2)
         for quadrant in range(4):
             nc.sync.dma_start(
-                out=w_scales[32 * quadrant : 32 * quadrant + 4, :].bitcast(I32),
+                out=scales_in[32 * quadrant : 32 * quadrant + 4, :].bitcast(I32),
                 in_=weight_scales[0, 4 * quadrant : 4 * quadrant + 4, :].bitcast(I32),
             )
-        nc.sync.dma_start(out=w_words[:].bitcast(I32), in_=weight_words[0].bitcast(I32))
+        nc.sync.dma_start(out=words_in[:].bitcast(I32), in_=weight_words[0].bitcast(I32))
         load_x(2, 2)
         for first in range(LOAD_BLOCKS, BLOCKS, LOAD_BLOCKS):
             load_x(first, LOAD_BLOCKS)
+
+        w_scales = keep.tile([P, N], U8, align_bytes=64)
+        nc.vector.tensor_copy(
+            out=w_scales[:].rearrange("p (b g e) -> p g b e", b=2, e=2),
+            in_=scales_in[:].rearrange("p (g b e) -> p g b e", b=2, e=2),
+        )
+        w_words = keep.tile([P, 2 * N], U8, align_bytes=64)
+        nc.vector.tensor_copy(
+            out=w_words[:].bitcast(I32).rearrange("p (b g) -> p b g", b=2),
+            in_=words_in[:].bitcast(I32).rearrange("p (g b) -> p b g", b=2),
+        )
 
         x_codes = keep.tile([P, BLOCKS * P], U32, align_bytes=64)
         x_scales = keep.tile([P, BLOCKS * P], U8, align_bytes=64)
@@ -83,7 +96,8 @@ def tile_mylayerfunc_kernel(tc, x, weight_words, weight_scales, out):
                 for u in range(2):
                     nc.tensor.transpose(out=xt[:, i, u, :], in_=words[:, u:WORDS:2], identity=ident[:])
             grouped = stage.tile([P, 2 * P * 4], BF16, align_bytes=64)
-            nc.scalar.copy(
+            copy = nc.vector.tensor_copy if 0 < first <= VECTOR_COPIES_UP_TO else nc.scalar.copy
+            copy(
                 out=grouped[:].bitcast(F32).rearrange("p (i r u) -> p i r u", i=2, u=2),
                 in_=xt[:].rearrange("p i u r -> p i r u"),
             )
@@ -96,84 +110,80 @@ def tile_mylayerfunc_kernel(tc, x, weight_words, weight_scales, out):
             )
 
         def multiply_and_functions(m):
-            planes = work.tile([P, 6, HALVES, PER_BANK], F32)
-            abs_y = work.tile([P, 2 * HALVES, PER_BANK], F32)
+            planes = work.tile([P, 6, GROUPS], F32)
+            abs_y = work.tile([P, 2, GROUPS], F32)
             rows = slice(m * P, (m + 1) * P)
-            by_kind = []
-            for h in range(HALVES):
+            banks = {}
+            for b in (1, 0):
                 y = psum_y.tile([P, BANK], F32)
                 nc.tensor.matmul_mx(
                     out=y[:],
                     lhsT=x_codes[:, rows].bitcast(FP8X4),
                     lhsT_scale=x_scales[:, rows],
-                    rhs=w_words[:, 2 * BANK * h : 2 * BANK * (h + 1)].bitcast(FP4X4),
-                    rhs_scale=w_scales[:, BANK * h : BANK * (h + 1)],
+                    rhs=w_words[:, 2 * BANK * b : 2 * BANK * (b + 1)].bitcast(FP4X4),
+                    rhs_scale=w_scales[:, BANK * b : BANK * (b + 1)],
                     start=True,
                     stop=True,
                 )
-                by_kind.append(y[:].rearrange("p (j c) -> p c j", c=KINDS))
-            def sines(h):
-                nc.scalar.activation(out=planes[:, SIN : SIN_T + 1 : 3, h, :], in_=by_kind[h][:, SIN : TAN + 1, :], func=ACT.Sin)
-
-            nc.scalar.activation(out=abs_y[:, 0:4:3, :], in_=by_kind[0][:, COS : TAN + 1 : 2, :], func=ACT.Abs)
-            nc.scalar.activation(out=abs_y[:, 1:3, :], in_=by_kind[1][:, COS : TAN + 1 : 2, :], func=ACT.Abs)
-            sines(0)
+                banks[b] = y[:].rearrange("p (g e) -> p e g", e=2)
+            nc.scalar.activation(out=abs_y[:, 1, :], in_=banks[1][:, 1, :], func=ACT.Abs)
+            nc.scalar.activation(out=abs_y[:, 0, :], in_=banks[0][:, 1, :], func=ACT.Abs)
+            nc.scalar.activation(out=planes[:, SIN : SIN_T + 1 : 3, :], in_=banks[1], func=ACT.Sin)
             nc.scalar.activation(
-                out=planes[:, COS : COS_T + 1 : 3, :, :],
-                in_=abs_y[:].rearrange("p (c h) j -> p c h j", h=HALVES),
-                func=ACT.Sin, bias=math.pi / 2, scale=-1.0
+                out=planes[:, COS : COS_T + 1 : 3, :], in_=abs_y[:], func=ACT.Sin, bias=math.pi / 2, scale=-1.0
             )
-            sines(1)
-            for h in range(HALVES):
-                nc.scalar.copy(out=planes[:, LIN, h, :], in_=by_kind[h][:, LIN, :])
+            nc.scalar.copy(out=planes[:, LIN, :], in_=banks[0][:, 0, :])
             planes_of[m] = planes
 
+        def halves(plane):
+            return plane.rearrange("p (h j) -> p h j", h=2)
+
         def products_up(m):
-            planes = planes_of[m]
-            pair = small.tile([P, 2, PER_BANK // 2], F32)
-            nc.vector.tensor_mul(
-                out=pair[:].rearrange("p q i -> p (q i)"), in0=planes[:, COS_T, 0, :], in1=planes[:, COS_T, 1, :]
-            )
+            cos_t = halves(planes_of[m][:, COS_T, :])
+            pair = small.tile([P, 2, QUARTER], F32)
+            nc.vector.tensor_mul(out=pair[:].rearrange("p q i -> p (q i)"), in0=cos_t[:, 0, :], in1=cos_t[:, 1, :])
             pair_of[m] = pair
 
         def product_of_four(m):
             pair = pair_of[m]
-            quad = small.tile([P, PER_BANK // 2], F32)
+            quad = small.tile([P, QUARTER], F32)
             nc.vector.tensor_mul(out=quad[:], in0=pair[:, 0, :], in1=pair[:, 1, :])
             quad_of[m] = quad
 
         def reciprocal(m):
-            inv_quad = small.tile([P, PER_BANK // 2], F32)
+            inv_quad = small.tile([P, QUARTER], F32)
             nc.vector.reciprocal(out=inv_quad[:], in_=quad_of[m][:])
             inv_quad_of[m] = inv_quad
 
         def cross_product(m):
             planes = planes_of[m]
-            cross = small.tile([P, HALVES, PER_BANK], F32)
-            nc.vector.tensor_mul(out=cross[:], in0=planes[:, SIN_T, :, :], in1=planes[:, COS_T, :, :])
+            cross = small.tile([P, 2, HALF], F32)
+            nc.vector.tensor_mul(
+                out=cross[:], in0=halves(planes[:, SIN_T, :]), in1=halves(planes[:, COS_T, :])[:, ::-1, :]
+            )
             cross_of[m] = cross
 
         def products_down(m):
-            inv_pair = small.tile([P, 2, PER_BANK // 2], F32)
+            inv_pair = small.tile([P, 2, QUARTER], F32)
             nc.vector.tensor_mul(
                 out=inv_pair[:],
-                in0=inv_quad_of[m][:].unsqueeze(1).to_broadcast([P, 2, PER_BANK // 2]),
+                in0=inv_quad_of[m][:].unsqueeze(1).to_broadcast([P, 2, QUARTER]),
                 in1=pair_of[m][:, ::-1, :],
             )
             inv_pair_of[m] = inv_pair
 
         def tangent(m):
             nc.vector.tensor_mul(
-                out=planes_of[m][:, TAN, :, :],
+                out=halves(planes_of[m][:, TAN, :]),
                 in0=cross_of[m][:],
-                in1=inv_pair_of[m][:].rearrange("p q i -> p (q i)").unsqueeze(1).to_broadcast([P, HALVES, PER_BANK]),
+                in1=inv_pair_of[m][:].rearrange("p q i -> p (q i)").unsqueeze(1).to_broadcast([P, 2, HALF]),
             )
 
         def weave_and_store(m, h):
             woven = work.tile([P, BANK], F32)
             nc.vector.tensor_copy(
                 out=woven[:].rearrange("p (j c) -> p j c", c=KINDS),
-                in_=planes_of[m][:, LIN : TAN + 1, h, :].rearrange("p c j -> p j c"),
+                in_=planes_of[m][:, LIN : TAN + 1, HALF * h : HALF * (h + 1)].rearrange("p c j -> p j c"),
             )
             nc.sync.dma_start(out=out_blocks[:, m, BANK * h : BANK * (h + 1)], in_=woven[:])
 

@@ -182,8 +182,8 @@ def tile_mylayerfunc_kernel(tc, x, weight_words, weight_scales, out):
         def weave_and_store(m, h):
             woven = work.tile([P, BANK], F32)
             nc.vector.tensor_copy(
-                out=woven[:].rearrange("p (j c) -> p j c", c=KINDS),
-                in_=planes_of[m][:, LIN : TAN + 1, HALF * h : HALF * (h + 1)].rearrange("p c j -> p j c"),
+                out=woven[:].rearrange("p (t i c) -> p t c i", i=4, c=KINDS),
+                in_=planes_of[m][:, LIN : TAN + 1, HALF * h : HALF * (h + 1)].rearrange("p c (t i) -> p t c i", i=4),
             )
             nc.sync.dma_start(out=out_blocks[:, m, BANK * h : BANK * (h + 1)], in_=woven[:])
 

@@ -60,22 +60,24 @@ def tile_mylayerfunc_kernel(tc, x, weight_words, weight_scales, out):
             blocks = slice(first, first + count)
             nc.sync.dma_start(out=x_sb[:, blocks, :], in_=x_blocks[:, blocks, :])
 
-        load_x(0, 2)
+        load_x(0, 1)
         for quadrant in range(4):
             nc.sync.dma_start(
                 out=scales_in[32 * quadrant : 32 * quadrant + 4, :].bitcast(I32),
                 in_=weight_scales[0, 4 * quadrant : 4 * quadrant + 4, :].bitcast(I32),
             )
         nc.sync.dma_start(out=words_in[:].bitcast(I32), in_=weight_words[0].bitcast(I32))
+        load_x(1, 1)
         load_x(2, 2)
         for first in range(LOAD_BLOCKS, BLOCKS, LOAD_BLOCKS):
             load_x(first, LOAD_BLOCKS)
 
         w_scales = keep.tile([P, N], U8, align_bytes=64)
-        nc.vector.tensor_copy(
-            out=w_scales[:].rearrange("p (b g e) -> p g b e", b=2, e=2),
-            in_=scales_in[:].rearrange("p (g b e) -> p g b e", b=2, e=2),
-        )
+        for b in (1, 0):
+            nc.vector.tensor_copy(
+                out=w_scales[:, BANK * b : BANK * (b + 1)].rearrange("p (g e) -> p g e", e=2),
+                in_=scales_in[:].rearrange("p (g b e) -> p b g e", b=2, e=2)[:, b, :, :],
+            )
         w_words = keep.tile([P, 2 * N], U8, align_bytes=64)
         nc.vector.tensor_copy(
             out=w_words[:].bitcast(I32).rearrange("p (b g) -> p b g", b=2),
@@ -86,25 +88,25 @@ def tile_mylayerfunc_kernel(tc, x, weight_words, weight_scales, out):
         x_scales = keep.tile([P, BLOCKS * P], U8, align_bytes=64)
 
         grouped_of = {}
-        planes_of = {}
+        planes_of, abs_of, linear_of = {}, {}, {}
         pair_of, quad_of, inv_quad_of, inv_pair_of, cross_of = {}, {}, {}, {}, {}
 
-        def transpose_two_blocks(first):
-            xt = psum_x.tile([P, 2, 2, P], F32)
-            for i in range(2):
+        def transpose_blocks(first, count):
+            xt = psum_x.tile([P, count, 2, P], F32)
+            for i in range(count):
                 words = x_sb[:, first + i, :].bitcast(F32)
                 for u in range(2):
                     nc.tensor.transpose(out=xt[:, i, u, :], in_=words[:, u:WORDS:2], identity=ident[:])
-            grouped = stage.tile([P, 2 * P * 4], BF16, align_bytes=64)
-            copy = nc.vector.tensor_copy if 0 < first <= VECTOR_COPIES_UP_TO else nc.scalar.copy
+            grouped = stage.tile([P, count * P * 4], BF16, align_bytes=64)
+            copy = nc.vector.tensor_copy if 2 <= first <= VECTOR_COPIES_UP_TO else nc.scalar.copy
             copy(
-                out=grouped[:].bitcast(F32).rearrange("p (i r u) -> p i r u", i=2, u=2),
+                out=grouped[:].bitcast(F32).rearrange("p (i r u) -> p i r u", i=count, u=2),
                 in_=xt[:].rearrange("p i u r -> p i r u"),
             )
             grouped_of[first] = grouped
 
-        def quantise_two_blocks(first):
-            cols = slice(first * P, (first + 2) * P)
+        def quantise_blocks(first, count):
+            cols = slice(first * P, (first + count) * P)
             nc.vector.quantize_mx(
                 out=x_codes[:, cols].bitcast(FP8X4), scales=x_scales[:, cols], in_=grouped_of[first][:]
             )
@@ -128,12 +130,18 @@ def tile_mylayerfunc_kernel(tc, x, weight_words, weight_scales, out):
                 banks[b] = y[:].rearrange("p (g e) -> p e g", e=2)
             nc.scalar.activation(out=abs_y[:, 1, :], in_=banks[1][:, 1, :], func=ACT.Abs)
             nc.scalar.activation(out=abs_y[:, 0, :], in_=banks[0][:, 1, :], func=ACT.Abs)
+            cosine(planes, abs_y, COS_T, 1)
             nc.scalar.activation(out=planes[:, SIN : SIN_T + 1 : 3, :], in_=banks[1], func=ACT.Sin)
+            planes_of[m], abs_of[m], linear_of[m] = planes, abs_y, banks[0][:, 0, :]
+
+        def cosine(planes, abs_y, plane, slot):
             nc.scalar.activation(
-                out=planes[:, COS : COS_T + 1 : 3, :], in_=abs_y[:], func=ACT.Sin, bias=math.pi / 2, scale=-1.0
+                out=planes[:, plane, :], in_=abs_y[:, slot, :], func=ACT.Sin, bias=math.pi / 2, scale=-1.0
             )
-            nc.scalar.copy(out=planes[:, LIN, :], in_=banks[0][:, 0, :])
-            planes_of[m] = planes
+
+        def cos_and_linear(m):
+            cosine(planes_of[m], abs_of[m], COS, 0)
+            nc.scalar.copy(out=planes_of[m][:, LIN, :], in_=linear_of[m])
 
         def halves(plane):
             return plane.rearrange("p (h j) -> p h j", h=2)
@@ -187,15 +195,19 @@ def tile_mylayerfunc_kernel(tc, x, weight_words, weight_scales, out):
             )
             nc.sync.dma_start(out=out_blocks[:, m, BANK * h : BANK * (h + 1)], in_=woven[:])
 
-        transpose_two_blocks(0)
-        quantise_two_blocks(0)
+        for first in range(2):
+            transpose_blocks(first, 1)
+            quantise_blocks(first, 1)
         for m in range(BLOCKS + 2):
             more_x = 2 * m + 2 < BLOCKS
             going_up, going_down, weaving = m < BLOCKS, 1 <= m <= BLOCKS, m >= 2
             if going_up:
                 multiply_and_functions(m)
+            if going_down:
+                cos_and_linear(m - 1)
+            if going_up:
                 if more_x:
-                    transpose_two_blocks(2 * m + 2)
+                    transpose_blocks(2 * m + 2, 2)
             if weaving:
                 weave_and_store(m - 2, 0)
             if going_down:
@@ -211,4 +223,4 @@ def tile_mylayerfunc_kernel(tc, x, weight_words, weight_scales, out):
                 cross_product(m)
                 reciprocal(m)
             if more_x:
-                quantise_two_blocks(2 * m + 2)
+                quantise_blocks(2 * m + 2, 2)

@@ -210,17 +210,18 @@ def tile_mylayerfunc_kernel(tc, x, weight_words, weight_scales, out):
                     transpose_blocks(2 * m + 2, 2)
             if weaving:
                 weave_and_store(m - 2, 0)
+            if going_up:
+                products_up(m)
             if going_down:
                 products_down(m - 1)
             if weaving:
                 weave_and_store(m - 2, 1)
             if going_up:
-                products_up(m)
+                product_of_four(m)
+                cross_product(m)
             if going_down:
                 tangent(m - 1)
             if going_up:
-                product_of_four(m)
-                cross_product(m)
                 reciprocal(m)
             if more_x:
                 quantise_blocks(2 * m + 2, 2)

@@ -23,6 +23,7 @@ HALF = GROUPS // 2
 QUARTER = GROUPS // 4
 WORDS = K // 2
 LOAD_BLOCKS = 4
+WARM_UP_MATMULS = 4
 VECTOR_COPIES_UP_TO = 6
 
 LIN, COS, SIN, TAN, COS_T, SIN_T = 0, 1, 2, 3, 4, 5
@@ -52,6 +53,12 @@ def tile_mylayerfunc_kernel(tc, x, weight_words, weight_scales, out):
         nc.vector.memset(scales_in[:].bitcast(I32), 0)
         ident = keep.tile([P, P], F32)
         make_identity(nc, ident[:])
+
+        zeros = keep.tile([P, BANK], BF16)
+        nc.vector.memset(zeros[:], 0.0)
+        idle_sums = psum_y.tile([P, BANK], F32, name="y")
+        for repeat in range(WARM_UP_MATMULS):
+            nc.tensor.matmul(out=idle_sums[:], lhsT=zeros[:, 0:P], rhs=zeros[:], start=True, stop=True)
 
         x_sb = keep.tile([P, BLOCKS, K], BF16)
         words_in = keep.tile([P, 2 * N], U8, align_bytes=64)

@@ -11,6 +11,7 @@ U32 = mybir.dt.uint32
 U8 = mybir.dt.uint8
 FP8X4 = mybir.dt.float8_e4m3fn_x4
 FP4X4 = mybir.dt.float4_e2m1fn_x4
+ALU = mybir.AluOpType
 ACT = mybir.ActivationFunctionType
 
 P = 128
@@ -20,13 +21,14 @@ BANK = 512
 KINDS = 4
 GROUPS = N // KINDS
 HALF = GROUPS // 2
-QUARTER = GROUPS // 4
 WORDS = K // 2
 LOAD_BLOCKS = 4
 WARM_UP_MATMULS = 4
 VECTOR_COPIES_UP_TO = 6
 
 LIN, COS, SIN, TAN, COS_T, SIN_T = 0, 1, 2, 3, 4, 5
+
+SCALE = float(2**24)
 
 FLOPS = 2 * B * K * N
 
@@ -96,7 +98,7 @@ def tile_mylayerfunc_kernel(tc, x, weight_words, weight_scales, out):
 
         grouped_of = {}
         planes_of, abs_of, linear_of = {}, {}, {}
-        pair_of, quad_of, inv_quad_of, inv_pair_of, cross_of = {}, {}, {}, {}, {}
+        products_of, inverse_of, cross_of = {}, {}, {}
 
         def transpose_blocks(first, count):
             xt = psum_x.tile([P, count, 2, P], F32)
@@ -153,22 +155,29 @@ def tile_mylayerfunc_kernel(tc, x, weight_words, weight_scales, out):
         def halves(plane):
             return plane.rearrange("p (h j) -> p h j", h=2)
 
-        def products_up(m):
-            cos_t = halves(planes_of[m][:, COS_T, :])
-            pair = small.tile([P, 2, QUARTER], F32)
-            nc.vector.tensor_mul(out=pair[:].rearrange("p q i -> p (q i)"), in0=cos_t[:, 0, :], in1=cos_t[:, 1, :])
-            pair_of[m] = pair
+        def levels(m):
+            return 3 if m < BLOCKS - 2 else 2
 
-        def product_of_four(m):
-            pair = pair_of[m]
-            quad = small.tile([P, QUARTER], F32)
-            nc.vector.tensor_mul(out=quad[:], in0=pair[:, 0, :], in1=pair[:, 1, :])
-            quad_of[m] = quad
+        def product_up(m, level):
+            if level == 0:
+                products_of[m] = [halves(planes_of[m][:, COS_T, :])]
+            if level >= levels(m):
+                return
+            above = products_of[m][level]
+            product = small.tile([P, GROUPS // 2 ** (level + 1)], F32, name="product" + str(level))
+            if level == 0:
+                nc.vector.scalar_tensor_tensor(
+                    out=product[:], in0=above[:, 0, :], scalar=SCALE, in1=above[:, 1, :], op0=ALU.mult, op1=ALU.mult
+                )
+            else:
+                nc.vector.tensor_mul(out=product[:], in0=above[:, 0, :], in1=above[:, 1, :])
+            products_of[m].append(halves(product[:]))
+            inverse_of[m] = product[:]
 
         def reciprocal(m):
-            inv_quad = small.tile([P, QUARTER], F32)
-            nc.vector.reciprocal(out=inv_quad[:], in_=quad_of[m][:])
-            inv_quad_of[m] = inv_quad
+            inverse = small.tile([P, GROUPS // 2 ** levels(m)], F32)
+            nc.vector.reciprocal(out=inverse[:], in_=inverse_of[m])
+            inverse_of[m] = inverse[:]
 
         def cross_product(m):
             planes = planes_of[m]
@@ -178,20 +187,26 @@ def tile_mylayerfunc_kernel(tc, x, weight_words, weight_scales, out):
             )
             cross_of[m] = cross
 
-        def products_down(m):
-            inv_pair = small.tile([P, 2, QUARTER], F32)
+        def product_down(m, level):
+            if level >= levels(m):
+                return
+            width = GROUPS // 2 ** (level + 1)
+            inverse = small.tile([P, 2, width], F32, name="inverse" + str(level))
             nc.vector.tensor_mul(
-                out=inv_pair[:],
-                in0=inv_quad_of[m][:].unsqueeze(1).to_broadcast([P, 2, QUARTER]),
-                in1=pair_of[m][:, ::-1, :],
+                out=inverse[:],
+                in0=inverse_of[m].unsqueeze(1).to_broadcast([P, 2, width]),
+                in1=products_of[m][level][:, ::-1, :],
             )
-            inv_pair_of[m] = inv_pair
+            inverse_of[m] = inverse[:].rearrange("p q i -> p (q i)")
 
         def tangent(m):
-            nc.vector.tensor_mul(
+            nc.vector.scalar_tensor_tensor(
                 out=halves(planes_of[m][:, TAN, :]),
                 in0=cross_of[m][:],
-                in1=inv_pair_of[m][:].rearrange("p q i -> p (q i)").unsqueeze(1).to_broadcast([P, 2, HALF]),
+                scalar=SCALE,
+                in1=inverse_of[m].unsqueeze(1).to_broadcast([P, 2, HALF]),
+                op0=ALU.mult,
+                op1=ALU.mult,
             )
 
         def weave_and_store(m, h):
@@ -212,23 +227,26 @@ def tile_mylayerfunc_kernel(tc, x, weight_words, weight_scales, out):
                 multiply_and_functions(m)
             if going_down:
                 cos_and_linear(m - 1)
+            if more_x:
+                transpose_blocks(2 * m + 2, 2)
             if going_up:
-                if more_x:
-                    transpose_blocks(2 * m + 2, 2)
+                product_up(m, 0)
             if weaving:
                 weave_and_store(m - 2, 0)
-            if going_up:
-                products_up(m)
             if going_down:
-                products_down(m - 1)
+                product_down(m - 1, 2)
+            if going_up:
+                cross_product(m)
+                product_up(m, 1)
+            if going_down:
+                product_down(m - 1, 1)
             if weaving:
                 weave_and_store(m - 2, 1)
+            if more_x:
+                quantise_blocks(2 * m + 2, 2)
             if going_up:
-                product_of_four(m)
-                cross_product(m)
+                product_up(m, 2)
             if going_down:
                 tangent(m - 1)
             if going_up:
                 reciprocal(m)
-            if more_x:
-                quantise_blocks(2 * m + 2, 2)

@@ -24,7 +24,7 @@ HALF = GROUPS // 2
 WORDS = K // 2
 LOAD_BLOCKS = 4
 WARM_UP_MATMULS = 4
-VECTOR_COPIES_UP_TO = 6
+VECTOR_COPIES_UP_TO = 8
 
 LIN, COS, SIN, TAN, COS_T, SIN_T = 0, 1, 2, 3, 4, 5
 
@@ -212,8 +212,10 @@ def tile_mylayerfunc_kernel(tc, x, weight_words, weight_scales, out):
         def weave_and_store(m, h):
             woven = work.tile([P, BANK], F32)
             nc.vector.tensor_copy(
-                out=woven[:].rearrange("p (t i c) -> p t c i", i=4, c=KINDS),
-                in_=planes_of[m][:, LIN : TAN + 1, HALF * h : HALF * (h + 1)].rearrange("p c (t i) -> p t c i", i=4),
+                out=woven[:].rearrange("p (t i d c) -> p t d i c", i=4, d=2, c=2),
+                in_=planes_of[m][:, LIN : TAN + 1, HALF * h : HALF * (h + 1)].rearrange(
+                    "p (d c) (t i) -> p t d i c", c=2, i=4
+                ),
             )
             nc.sync.dma_start(out=out_blocks[:, m, BANK * h : BANK * (h + 1)], in_=woven[:])
 

@@ -24,9 +24,11 @@ HALF = GROUPS // 2
 WORDS = K // 2
 LOAD_BLOCKS = 4
 WARM_UP_MATMULS = 4
-VECTOR_COPIES_UP_TO = 8
+VECTOR_COPIES_UP_TO = 6
 
 LIN, COS, SIN, TAN, COS_T, SIN_T = 0, 1, 2, 3, 4, 5
+PLANES = 6
+COS_STEP = PLANES + COS_T - COS
 
 SCALE = float(2**24)
 
@@ -42,7 +44,8 @@ def tile_mylayerfunc_kernel(tc, x, weight_words, weight_scales, out):
         ctx.enter_context(tc.manual_schedule())
         keep = ctx.enter_context(tc.tile_pool(name="keep", bufs=1))
         stage = ctx.enter_context(tc.tile_pool(name="stage", bufs=2))
-        work = ctx.enter_context(tc.tile_pool(name="work", bufs=6))
+        magnitudes = ctx.enter_context(tc.tile_pool(name="magnitudes", bufs=6))
+        store = ctx.enter_context(tc.tile_pool(name="store", bufs=2 * BLOCKS))
         small = ctx.enter_context(tc.tile_pool(name="small", bufs=4))
         psum_x = ctx.enter_context(tc.psum_pool(name="psum_x", bufs=2))
         psum_y = ctx.enter_context(tc.psum_pool(name="psum_y", bufs=6))
@@ -93,6 +96,7 @@ def tile_mylayerfunc_kernel(tc, x, weight_words, weight_scales, out):
             in_=words_in[:].bitcast(I32).rearrange("p (g b) -> p b g", b=2),
         )
 
+        all_planes = keep.tile([P, BLOCKS * PLANES, GROUPS], F32)
         x_codes = keep.tile([P, BLOCKS * P], U32, align_bytes=64)
         x_scales = keep.tile([P, BLOCKS * P], U8, align_bytes=64)
 
@@ -121,8 +125,10 @@ def tile_mylayerfunc_kernel(tc, x, weight_words, weight_scales, out):
             )
 
         def multiply_and_functions(m):
-            planes = work.tile([P, 6, GROUPS], F32)
-            abs_y = work.tile([P, 2, GROUPS], F32)
+            planes = all_planes[:, PLANES * m : PLANES * (m + 1), :]
+            if m == 0:
+                abs_of[0] = magnitudes.tile([P, 2, GROUPS], F32, name="abs_y")
+            abs_of[m + 1] = magnitudes.tile([P, 2, GROUPS], F32, name="abs_y")
             rows = slice(m * P, (m + 1) * P)
             banks = {}
             for b in (1, 0):
@@ -137,19 +143,26 @@ def tile_mylayerfunc_kernel(tc, x, weight_words, weight_scales, out):
                     stop=True,
                 )
                 banks[b] = y[:].rearrange("p (g e) -> p e g", e=2)
-            nc.scalar.activation(out=abs_y[:, 1, :], in_=banks[1][:, 1, :], func=ACT.Abs)
-            nc.scalar.activation(out=abs_y[:, 0, :], in_=banks[0][:, 1, :], func=ACT.Abs)
-            cosine(planes, abs_y, COS_T, 1)
+            nc.scalar.activation(out=abs_of[m][:, 1, :], in_=banks[1][:, 1, :], func=ACT.Abs)
+            nc.scalar.activation(out=abs_of[m + 1][:, 0, :], in_=banks[0][:, 1, :], func=ACT.Abs)
+            cosines(m, 1 if m in (0, BLOCKS - 1) else 0, 2)
             nc.scalar.activation(out=planes[:, SIN : SIN_T + 1 : 3, :], in_=banks[1], func=ACT.Sin)
-            planes_of[m], abs_of[m], linear_of[m] = planes, abs_y, banks[0][:, 0, :]
+            if m == BLOCKS - 1:
+                cosines(m, 0, 1)
+            planes_of[m], linear_of[m] = planes, banks[0][:, 0, :]
 
-        def cosine(planes, abs_y, plane, slot):
+        def cosines(m, begin, end):
+            first = PLANES * (m - 1) + COS + COS_STEP * begin
+            last = PLANES * (m - 1) + COS + COS_STEP * (end - 1)
             nc.scalar.activation(
-                out=planes[:, plane, :], in_=abs_y[:, slot, :], func=ACT.Sin, bias=math.pi / 2, scale=-1.0
+                out=all_planes[:, first : last + 1 : COS_STEP, :],
+                in_=abs_of[m][:, begin:end, :],
+                func=ACT.Sin,
+                bias=math.pi / 2,
+                scale=-1.0,
             )
 
-        def cos_and_linear(m):
-            cosine(planes_of[m], abs_of[m], COS, 0)
+        def linear(m):
             nc.scalar.copy(out=planes_of[m][:, LIN, :], in_=linear_of[m])
 
         def halves(plane):
@@ -210,7 +223,7 @@ def tile_mylayerfunc_kernel(tc, x, weight_words, weight_scales, out):
             )
 
         def weave_and_store(m, h):
-            woven = work.tile([P, BANK], F32)
+            woven = store.tile([P, BANK], F32)
             nc.vector.tensor_copy(
                 out=woven[:].rearrange("p (t i d c) -> p t d i c", i=4, d=2, c=2),
                 in_=planes_of[m][:, LIN : TAN + 1, HALF * h : HALF * (h + 1)].rearrange(
@@ -227,8 +240,10 @@ def tile_mylayerfunc_kernel(tc, x, weight_words, weight_scales, out):
             going_up, going_down, weaving = m < BLOCKS, 1 <= m <= BLOCKS, m >= 2
             if going_up:
                 multiply_and_functions(m)
+            if m == BLOCKS:
+                cosines(BLOCKS, 0, 1)
             if going_down:
-                cos_and_linear(m - 1)
+                linear(m - 1)
             if more_x:
                 transpose_blocks(2 * m + 2, 2)
             if going_up:

@@ -23,7 +23,7 @@ GROUPS = N // KINDS
 HALF = GROUPS // 2
 WORDS = K // 2
 LOAD_BLOCKS = 4
-WARM_UP_MATMULS = 4
+WARM_UP_MATMULS = 3
 VECTOR_COPIES_UP_TO = 6
 
 LIN, COS, SIN, TAN, COS_T, SIN_T = 0, 1, 2, 3, 4, 5
@@ -43,8 +43,8 @@ def tile_mylayerfunc_kernel(tc, x, weight_words, weight_scales, out):
     with ExitStack() as ctx:
         ctx.enter_context(tc.manual_schedule())
         keep = ctx.enter_context(tc.tile_pool(name="keep", bufs=1))
-        stage = ctx.enter_context(tc.tile_pool(name="stage", bufs=2))
-        magnitudes = ctx.enter_context(tc.tile_pool(name="magnitudes", bufs=6))
+        stage = ctx.enter_context(tc.tile_pool(name="stage", bufs=9))
+        magnitudes = ctx.enter_context(tc.tile_pool(name="magnitudes", bufs=8))
         store = ctx.enter_context(tc.tile_pool(name="store", bufs=2 * BLOCKS))
         small = ctx.enter_context(tc.tile_pool(name="small", bufs=4))
         psum_x = ctx.enter_context(tc.psum_pool(name="psum_x", bufs=2))
@@ -59,11 +59,16 @@ def tile_mylayerfunc_kernel(tc, x, weight_words, weight_scales, out):
         ident = keep.tile([P, P], F32)
         make_identity(nc, ident[:])
 
-        zeros = keep.tile([P, BANK], BF16)
-        nc.vector.memset(zeros[:], 0.0)
+        zero_words = keep.tile([P, BANK // 2], F32)
+        nc.vector.memset(zero_words[:], 0.0)
+        zeros = zero_words[:].bitcast(BF16)
         idle_sums = psum_y.tile([P, BANK], F32, name="y")
-        for repeat in range(WARM_UP_MATMULS):
-            nc.tensor.matmul(out=idle_sums[:], lhsT=zeros[:, 0:P], rhs=zeros[:], start=True, stop=True)
+
+        def multiply_zeros(count):
+            for repeat in range(count):
+                nc.tensor.matmul(out=idle_sums[:], lhsT=zeros[:, 0:P], rhs=zeros, start=True, stop=True)
+
+        multiply_zeros(WARM_UP_MATMULS)
 
         x_sb = keep.tile([P, BLOCKS, K], BF16)
         words_in = keep.tile([P, 2 * N], U8, align_bytes=64)
@@ -73,28 +78,29 @@ def tile_mylayerfunc_kernel(tc, x, weight_words, weight_scales, out):
             nc.sync.dma_start(out=x_sb[:, blocks, :], in_=x_blocks[:, blocks, :])
 
         load_x(0, 1)
+        nc.sync.dma_start(out=words_in[:].bitcast(I32), in_=weight_words[0].bitcast(I32))
         for quadrant in range(4):
             nc.sync.dma_start(
                 out=scales_in[32 * quadrant : 32 * quadrant + 4, :].bitcast(I32),
                 in_=weight_scales[0, 4 * quadrant : 4 * quadrant + 4, :].bitcast(I32),
             )
-        nc.sync.dma_start(out=words_in[:].bitcast(I32), in_=weight_words[0].bitcast(I32))
         load_x(1, 1)
         load_x(2, 2)
         for first in range(LOAD_BLOCKS, BLOCKS, LOAD_BLOCKS):
             load_x(first, LOAD_BLOCKS)
 
-        w_scales = keep.tile([P, N], U8, align_bytes=64)
-        for b in (1, 0):
-            nc.vector.tensor_copy(
-                out=w_scales[:, BANK * b : BANK * (b + 1)].rearrange("p (g e) -> p g e", e=2),
-                in_=scales_in[:].rearrange("p (g b e) -> p b g e", b=2, e=2)[:, b, :, :],
-            )
         w_words = keep.tile([P, 2 * N], U8, align_bytes=64)
         nc.vector.tensor_copy(
             out=w_words[:].bitcast(I32).rearrange("p (b g) -> p b g", b=2),
             in_=words_in[:].bitcast(I32).rearrange("p (g b) -> p b g", b=2),
         )
+        w_scales = keep.tile([P, N], U8, align_bytes=64)
+
+        def sort_scales(b):
+            nc.vector.tensor_copy(
+                out=w_scales[:, BANK * b : BANK * (b + 1)].rearrange("p (g e) -> p g e", e=2),
+                in_=scales_in[:].rearrange("p (g b e) -> p b g e", b=2, e=2)[:, b, :, :],
+            )
 
         all_planes = keep.tile([P, BLOCKS * PLANES, GROUPS], F32)
         x_codes = keep.tile([P, BLOCKS * P], U32, align_bytes=64)
@@ -232,9 +238,13 @@ def tile_mylayerfunc_kernel(tc, x, weight_words, weight_scales, out):
             )
             nc.sync.dma_start(out=out_blocks[:, m, BANK * h : BANK * (h + 1)], in_=woven[:])
 
-        for first in range(2):
-            transpose_blocks(first, 1)
-            quantise_blocks(first, 1)
+        sort_scales(1)
+        transpose_blocks(0, 1)
+        multiply_zeros(1)
+        quantise_blocks(0, 1)
+        sort_scales(0)
+        transpose_blocks(1, 1)
+        quantise_blocks(1, 1)
         for m in range(BLOCKS + 2):
             more_x = 2 * m + 2 < BLOCKS
             going_up, going_down, weaving = m < BLOCKS, 1 <= m <= BLOCKS, m >= 2

import math
from contextlib import ExitStack

import concourse.mybir as mybir
from concourse.masks import make_identity

F32 = mybir.dt.float32
BF16 = mybir.dt.bfloat16
I32 = mybir.dt.int32
U32 = mybir.dt.uint32
U8 = mybir.dt.uint8
FP8X4 = mybir.dt.float8_e4m3fn_x4
FP4X4 = mybir.dt.float4_e2m1fn_x4
ALU = mybir.AluOpType
ACT = mybir.ActivationFunctionType

P = 128
B, K, N = 2048, 512, 1024
BLOCKS = B // P
BANK = 512
KINDS = 4
GROUPS = N // KINDS
HALF = GROUPS // 2
WORDS = K // 2
LOAD_BLOCKS = 4
WARM_UP_MATMULS = 3
VECTOR_COPIES_UP_TO = 6

LIN, COS, SIN, TAN, COS_T, SIN_T = 0, 1, 2, 3, 4, 5
PLANES = 6
COS_STEP = PLANES + COS_T - COS

SCALE = float(2**24)

FLOPS = 2 * B * K * N


def tile_mylayerfunc_kernel(tc, x, weight_words, weight_scales, out):
    nc = tc.nc
    x_blocks = x.rearrange("(p m) k -> p m k", m=BLOCKS)
    out_blocks = out.rearrange("(p m) n -> p m n", m=BLOCKS)

    with ExitStack() as ctx:
        ctx.enter_context(tc.manual_schedule())
        keep = ctx.enter_context(tc.tile_pool(name="keep", bufs=1))
        stage = ctx.enter_context(tc.tile_pool(name="stage", bufs=9))
        magnitudes = ctx.enter_context(tc.tile_pool(name="magnitudes", bufs=8))
        store = ctx.enter_context(tc.tile_pool(name="store", bufs=2 * BLOCKS))
        small = ctx.enter_context(tc.tile_pool(name="small", bufs=4))
        psum_x = ctx.enter_context(tc.psum_pool(name="psum_x", bufs=2))
        psum_y = ctx.enter_context(tc.psum_pool(name="psum_y", bufs=6))

        table_warm = keep.tile([P, 1], F32)
        nc.vector.memset(table_warm[:], 0.0)
        nc.scalar.activation(out=table_warm[:], in_=table_warm[:], func=ACT.Sin)

        scales_in = keep.tile([P, N], U8, align_bytes=64)
        nc.vector.memset(scales_in[:].bitcast(I32), 0)
        ident = keep.tile([P, P], F32)
        make_identity(nc, ident[:])

        zero_words = keep.tile([P, BANK // 2], F32)
        nc.vector.memset(zero_words[:], 0.0)
        zeros = zero_words[:].bitcast(BF16)
        idle_sums = psum_y.tile([P, BANK], F32, name="y")

        def multiply_zeros(count):
            for repeat in range(count):
                nc.tensor.matmul(out=idle_sums[:], lhsT=zeros[:, 0:P], rhs=zeros, start=True, stop=True)

        multiply_zeros(WARM_UP_MATMULS)

        x_sb = keep.tile([P, BLOCKS, K], BF16)
        words_in = keep.tile([P, 2 * N], U8, align_bytes=64)

        def load_x(first, count):
            blocks = slice(first, first + count)
            nc.sync.dma_start(out=x_sb[:, blocks, :], in_=x_blocks[:, blocks, :])

        load_x(0, 1)
        nc.sync.dma_start(out=words_in[:].bitcast(I32), in_=weight_words[0].bitcast(I32))
        for quadrant in range(4):
            nc.sync.dma_start(
                out=scales_in[32 * quadrant : 32 * quadrant + 4, :].bitcast(I32),
                in_=weight_scales[0, 4 * quadrant : 4 * quadrant + 4, :].bitcast(I32),
            )
        load_x(1, 1)
        load_x(2, 2)
        for first in range(LOAD_BLOCKS, BLOCKS, LOAD_BLOCKS):
            load_x(first, LOAD_BLOCKS)

        w_words = keep.tile([P, 2 * N], U8, align_bytes=64)
        nc.vector.tensor_copy(
            out=w_words[:].bitcast(I32).rearrange("p (b g) -> p b g", b=2),
            in_=words_in[:].bitcast(I32).rearrange("p (g b) -> p b g", b=2),
        )
        w_scales = keep.tile([P, N], U8, align_bytes=64)

        def sort_scales(b):
            nc.vector.tensor_copy(
                out=w_scales[:, BANK * b : BANK * (b + 1)].rearrange("p (g e) -> p g e", e=2),
                in_=scales_in[:].rearrange("p (g b e) -> p b g e", b=2, e=2)[:, b, :, :],
            )

        all_planes = keep.tile([P, BLOCKS * PLANES, GROUPS], F32)
        x_codes = keep.tile([P, BLOCKS * P], U32, align_bytes=64)
        x_scales = keep.tile([P, BLOCKS * P], U8, align_bytes=64)

        grouped_of = {}
        planes_of, abs_of, linear_of = {}, {}, {}
        products_of, inverse_of, cross_of = {}, {}, {}

        def transpose_blocks(first, count):
            xt = psum_x.tile([P, count, 2, P], F32)
            for i in range(count):
                words = x_sb[:, first + i, :].bitcast(F32)
                for u in range(2):
                    nc.tensor.transpose(out=xt[:, i, u, :], in_=words[:, u:WORDS:2], identity=ident[:])
            grouped = stage.tile([P, count * P * 4], BF16, align_bytes=64)
            copy = nc.vector.tensor_copy if 2 <= first <= VECTOR_COPIES_UP_TO else nc.scalar.copy
            copy(
                out=grouped[:].bitcast(F32).rearrange("p (i r u) -> p i r u", i=count, u=2),
                in_=xt[:].rearrange("p i u r -> p i r u"),
            )
            grouped_of[first] = grouped

        def quantise_blocks(first, count):
            cols = slice(first * P, (first + count) * P)
            nc.vector.quantize_mx(
                out=x_codes[:, cols].bitcast(FP8X4), scales=x_scales[:, cols], in_=grouped_of[first][:]
            )

        def multiply_and_functions(m):
            planes = all_planes[:, PLANES * m : PLANES * (m + 1), :]
            if m == 0:
                abs_of[0] = magnitudes.tile([P, 2, GROUPS], F32, name="abs_y")
            abs_of[m + 1] = magnitudes.tile([P, 2, GROUPS], F32, name="abs_y")
            rows = slice(m * P, (m + 1) * P)
            banks = {}
            for b in (1, 0):
                y = psum_y.tile([P, BANK], F32)
                nc.tensor.matmul_mx(
                    out=y[:],
                    lhsT=x_codes[:, rows].bitcast(FP8X4),
                    lhsT_scale=x_scales[:, rows],
                    rhs=w_words[:, 2 * BANK * b : 2 * BANK * (b + 1)].bitcast(FP4X4),
                    rhs_scale=w_scales[:, BANK * b : BANK * (b + 1)],
                    start=True,
                    stop=True,
                )
                banks[b] = y[:].rearrange("p (g e) -> p e g", e=2)
            nc.scalar.activation(out=abs_of[m][:, 1, :], in_=banks[1][:, 1, :], func=ACT.Abs)
            nc.scalar.activation(out=abs_of[m + 1][:, 0, :], in_=banks[0][:, 1, :], func=ACT.Abs)
            cosines(m, 1 if m in (0, BLOCKS - 1) else 0, 2)
            nc.scalar.activation(out=planes[:, SIN : SIN_T + 1 : 3, :], in_=banks[1], func=ACT.Sin)
            if m == BLOCKS - 1:
                cosines(m, 0, 1)
            planes_of[m], linear_of[m] = planes, banks[0][:, 0, :]

        def cosines(m, begin, end):
            first = PLANES * (m - 1) + COS + COS_STEP * begin
            last = PLANES * (m - 1) + COS + COS_STEP * (end - 1)
            nc.scalar.activation(
                out=all_planes[:, first : last + 1 : COS_STEP, :],
                in_=abs_of[m][:, begin:end, :],
                func=ACT.Sin,
                bias=math.pi / 2,
                scale=-1.0,
            )

        def linear(m):
            nc.scalar.copy(out=planes_of[m][:, LIN, :], in_=linear_of[m])

        def halves(plane):
            return plane.rearrange("p (h j) -> p h j", h=2)

        def levels(m):
            return 3 if m < BLOCKS - 2 else 2

        def product_up(m, level):
            if level == 0:
                products_of[m] = [halves(planes_of[m][:, COS_T, :])]
            if level >= levels(m):
                return
            above = products_of[m][level]
            product = small.tile([P, GROUPS // 2 ** (level + 1)], F32, name="product" + str(level))
            if level == 0:
                nc.vector.scalar_tensor_tensor(
                    out=product[:], in0=above[:, 0, :], scalar=SCALE, in1=above[:, 1, :], op0=ALU.mult, op1=ALU.mult
                )
            else:
                nc.vector.tensor_mul(out=product[:], in0=above[:, 0, :], in1=above[:, 1, :])
            products_of[m].append(halves(product[:]))
            inverse_of[m] = product[:]

        def reciprocal(m):
            inverse = small.tile([P, GROUPS // 2 ** levels(m)], F32)
            nc.vector.reciprocal(out=inverse[:], in_=inverse_of[m])
            inverse_of[m] = inverse[:]

        def cross_product(m):
            planes = planes_of[m]
            cross = small.tile([P, 2, HALF], F32)
            nc.vector.tensor_mul(
                out=cross[:], in0=halves(planes[:, SIN_T, :]), in1=halves(planes[:, COS_T, :])[:, ::-1, :]
            )
            cross_of[m] = cross

        def product_down(m, level):
            if level >= levels(m):
                return
            width = GROUPS // 2 ** (level + 1)
            inverse = small.tile([P, 2, width], F32, name="inverse" + str(level))
            nc.vector.tensor_mul(
                out=inverse[:],
                in0=inverse_of[m].unsqueeze(1).to_broadcast([P, 2, width]),
                in1=products_of[m][level][:, ::-1, :],
            )
            inverse_of[m] = inverse[:].rearrange("p q i -> p (q i)")

        def tangent(m):
            nc.vector.scalar_tensor_tensor(
                out=halves(planes_of[m][:, TAN, :]),
                in0=cross_of[m][:],
                scalar=SCALE,
                in1=inverse_of[m].unsqueeze(1).to_broadcast([P, 2, HALF]),
                op0=ALU.mult,
                op1=ALU.mult,
            )

        def weave_and_store(m, h):
            woven = store.tile([P, BANK], F32)
            nc.vector.tensor_copy(
                out=woven[:].rearrange("p (t i d c) -> p t d i c", i=4, d=2, c=2),
                in_=planes_of[m][:, LIN : TAN + 1, HALF * h : HALF * (h + 1)].rearrange(
                    "p (d c) (t i) -> p t d i c", c=2, i=4
                ),
            )
            nc.sync.dma_start(out=out_blocks[:, m, BANK * h : BANK * (h + 1)], in_=woven[:])

        sort_scales(1)
        transpose_blocks(0, 1)
        multiply_zeros(1)
        quantise_blocks(0, 1)
        sort_scales(0)
        transpose_blocks(1, 1)
        quantise_blocks(1, 1)
        for m in range(BLOCKS + 2):
            more_x = 2 * m + 2 < BLOCKS
            going_up, going_down, weaving = m < BLOCKS, 1 <= m <= BLOCKS, m >= 2
            if going_up:
                multiply_and_functions(m)
            if m == BLOCKS:
                cosines(BLOCKS, 0, 1)
            if going_down:
                linear(m - 1)
            if more_x:
                transpose_blocks(2 * m + 2, 2)
            if going_up:
                product_up(m, 0)
            if weaving:
                weave_and_store(m - 2, 0)
            if going_down:
                product_down(m - 1, 2)
            if going_up:
                cross_product(m)
                product_up(m, 1)
            if going_down:
                product_down(m - 1, 1)
            if weaving:
                weave_and_store(m - 2, 1)
            if more_x:
                quantise_blocks(2 * m + 2, 2)
            if going_up:
                product_up(m, 2)
            if going_down:
                tangent(m - 1)
            if going_up:
                reciprocal(m)
